import numpy as np
import ml_dtypes


def mxq(x, axis, fmt="e4m3"):
    dtype, down = {"e4m3": (ml_dtypes.float8_e4m3fn, 7), "e5m2": (ml_dtypes.float8_e5m2, 14)}[fmt]
    v = np.moveaxis(np.asarray(x, np.float32).astype(ml_dtypes.bfloat16).astype(np.float64), axis, -1)
    blocks = v.reshape(v.shape[:-1] + (-1, 32))
    amax = np.abs(blocks).max(-1, keepdims=True)
    byte = np.maximum(np.where(amax > 0, np.frexp(amax)[1] - 1 + 127, 0) - down, 1)
    scale = np.exp2(byte - 127.0)
    codes = (blocks / scale).astype(np.float32).astype(dtype).astype(np.float64)
    return np.moveaxis((codes * scale).reshape(v.shape), -1, axis)


WIDE = False


def mx_kscale(k):
    if not WIDE:
        return np.ones(k)
    levels = np.array([10, -10, 5, -5, 0])
    if k % 512:
        return np.exp2(np.random.permutation(np.resize(levels, k // 32))).repeat(32)
    a = np.empty((k // 512, 16))
    for p in range(k // 512):
        a[p, :8] = np.random.permutation(np.resize(levels, 8))
        for g in range(8):
            far = levels[np.abs(levels - a[p, g]) >= 10]
            a[p, g + 8] = far[np.random.randint(len(far))]
    return np.exp2(a.ravel()).repeat(32)


BF16 = ml_dtypes.bfloat16


def bf(x):
    return np.asarray(x, np.float32).astype(BF16)


def f64(x):
    return np.asarray(x).astype(np.float64)


B, H, N, D, DT, NH = 32, 128, 128, 1024, 1024, 8


def softmax(v, axis):
    e = np.exp(v - v.max(axis=axis, keepdims=True))
    return e / e.sum(axis=axis, keepdims=True)


def draw0():
    s = mx_kscale(DT)
    return {"cand_topics": bf(np.random.standard_normal((B, N, DT)) * s),
            "Wq": bf(np.random.standard_normal((D, DT)) * 2.0 / np.sqrt(DT) / s[None, :]),
            "bq": bf(np.random.standard_normal(D) * 0.5)}


def core(cand_topics, Wq, bq):
    q = (mxq(f64(cand_topics), 2, "e4m3") @ mxq(f64(Wq), 1, "e4m3").T) + f64(bq)
    query_weights = softmax(np.sqrt((q ** 2).sum(axis=-1)), 1)
    return q, query_weights


def e4m3fn_bytes(y):
    return np.clip(np.asarray(y, np.float64), -448.0, 448.0).astype(np.float32).astype(ml_dtypes.float8_e4m3fn).view(np.uint8)


def e4m3fn_values(b):
    return np.asarray(b, np.uint8).view(ml_dtypes.float8_e4m3fn).astype(np.float64)


def setup_inputs():
    d = draw0()
    x0 = np.asarray(d['cand_topics']).astype(np.float64)
    s = (np.max(np.abs(x0), axis=(0, 1), keepdims=True) / 448.0).astype(np.float32)
    out = {}
    for k, v in d.items():
        if k == 'cand_topics':
            out['cand_topics_bytes'] = e4m3fn_bytes(x0 / s.astype(np.float64))
            out['cand_topics_scale'] = s
        else:
            out[k] = v
    return out


def reference(cand_topics_bytes, cand_topics_scale, Wq, bq):
    return core(e4m3fn_values(cand_topics_bytes) * cand_topics_scale.astype(np.float64), Wq, bq)

@@ -1,0 +1,309 @@
+from contextlib import ExitStack
+
+import concourse.masks as masks
+import concourse.mybir as mybir
+
+F32 = mybir.dt.float32
+BF16 = mybir.dt.bfloat16
+U32 = mybir.dt.uint32
+U8 = mybir.dt.uint8
+FP8 = mybir.dt.float8_e4m3fn
+FP8X4 = mybir.dt.float8_e4m3fn_x4
+ALU = mybir.AluOpType
+ACT = mybir.ActivationFunctionType
+AX = mybir.AxisListType
+
+B, N, K, D = 32, 128, 1024, 1024
+P = 128
+FLOPS = 2 * B * N * K * D
+
+PAIRS = B // 2
+CHUNKS = (2, 2, 4, 8, 8, 8)
+G_PAIRS = 10
+D_WIDEN = 6
+D_TRANSP = 5
+D_QUANT = 2
+
+
+def tile_candidateaware_clickednewsattention_pa_t_kernel(
+    tc, cand_topics_bytes, cand_topics_scale, Wq, bq, out_0, out_1
+):
+    nc = tc.nc
+    with ExitStack() as ctx:
+        const = ctx.enter_context(tc.tile_pool(name="const", bufs=1))
+        xs_pool = ctx.enter_context(tc.tile_pool(name="xs_pool", bufs=6))
+        xg_pool = ctx.enter_context(tc.tile_pool(name="xg_pool", bufs=4))
+        xq_pool = ctx.enter_context(tc.tile_pool(name="xq_pool", bufs=3))
+        q_pool = ctx.enter_context(tc.tile_pool(name="q_pool", bufs=3))
+        junk_pool = ctx.enter_context(tc.tile_pool(name="junk_pool", bufs=2))
+        psum_t = ctx.enter_context(tc.psum_pool(name="psum_t", bufs=4))
+        psum_a = ctx.enter_context(tc.psum_pool(name="psum_a", bufs=4))
+        ctx.enter_context(tc.manual_schedule())
+
+        scale2 = const.tile([P, 2, K], F32, name="scale2")
+        nc.sync.dma_start(
+            out=scale2[:, 0, :],
+            in_=cand_topics_scale.rearrange("a b k -> (a b k)").partition_broadcast(P),
+        )
+        xbytes = []
+        where = []
+        for c, n in enumerate(CHUNKS):
+            t = const.tile([P, n, K], U8, name="xbytes%d" % c)
+            xbytes.append(t)
+            for i in range(n):
+                where.append((c, i))
+        wraw = []
+        for c in range(4):
+            t = const.tile([P, 2, K], BF16, name="wraw%d" % c)
+            wraw.append(t)
+        bias_bc = const.tile([P, D], BF16, name="bias_bc")
+
+        def load_x(c):
+            b0 = sum(CHUNKS[:c])
+            nc.sync.dma_start(
+                out=xbytes[c][:],
+                in_=cand_topics_bytes[b0 : b0 + CHUNKS[c]].rearrange("b n k -> n b k"),
+            )
+
+        def load_w(c):
+            nc.sync.dma_start(
+                out=wraw[c][:],
+                in_=Wq[256 * c : 256 * (c + 1), :].rearrange("(c p) k -> p c k", p=P),
+            )
+
+        load_x(0)
+        load_w(0)
+        load_w(1)
+        load_x(1)
+        load_x(2)
+        load_w(2)
+        load_w(3)
+        load_x(3)
+        nc.sync.dma_start(out=bias_bc[:], in_=bq.partition_broadcast(P))
+        load_x(4)
+        load_x(5)
+
+        ident = const.tile([P, P], F32, name="ident")
+        masks.make_identity(nc, ident[:])
+        one_col = const.tile([P, 1], F32, name="one_col")
+        nc.vector.memset(one_col[:], 1.0)
+        r2_all = const.tile([P, P], F32, name="r2_all")
+        nc.vector.memset(r2_all[:], 1.0)
+        warm = const.tile([P, 2], F32, name="warm")
+        nc.scalar.activation(out=warm[:, 0:1], in_=one_col[:], func=ACT.Sqrt)
+        nc.scalar.copy(out=scale2[:, 1, :], in_=scale2[:, 0, :])
+
+        wgrp = []
+        wc = []
+        wsc = []
+        for h in range(2):
+            t = const.tile([P, 4 * K], BF16, name="wgrp%d" % h, align_bytes=64)
+            wgrp.append(t)
+            t = const.tile([P, K], U32, name="wc%d" % h, align_bytes=64)
+            wc.append(t)
+            t = const.tile([P, K], U8, name="wsc%d" % h, align_bytes=64)
+            wsc.append(t)
+
+        def transposes(words, base):
+            tp = psum_t.tile([P, 4, P], F32, name="tp")
+            for s in range(4):
+                g, u = divmod(s, 2)
+                lo = base + 256 * g
+                nc.tensor.transpose(tp[:, s, :], words[:, lo + u : lo + 256 : 2], ident[:])
+            return tp
+
+        def wprep(c):
+            h, cc = divmod(c, 4)
+            words = wraw[c // 2][:, c % 2, :].bitcast(F32)
+            tp = transposes(words, 0)
+            dst = wgrp[h][:].bitcast(F32).rearrange("p (g r u) -> p g r u", g=2, u=2)
+            nc.scalar.copy(
+                out=dst[:, :, cc * P : (cc + 1) * P, :],
+                in_=tp[:].rearrange("p (g u) r -> p g r u", u=2),
+            )
+
+        def quant_w(h):
+            nc.vector.quantize_mx(
+                out=wc[h][:].bitcast(FP8X4), scales=wsc[h][:], in_=wgrp[h][:]
+            )
+
+        xs_of = {}
+        xg_of = {}
+        xq_of = {}
+        acc_of = {}
+
+        def widen(j):
+            xs = xs_pool.tile([P, 2 * K], BF16, name="xs", align_bytes=64)
+            xs_of[j] = xs
+            c, i = where[2 * j]
+            if j == 0:
+                for a in range(2):
+                    nc.vector.tensor_tensor(
+                        out=xs[:, a * K : (a + 1) * K],
+                        in0=xbytes[c][:, i + a, :].bitcast(FP8),
+                        in1=scale2[:, 0, :],
+                        op=ALU.mult,
+                    )
+            else:
+                nc.vector.tensor_tensor(
+                    out=xs[:],
+                    in0=xbytes[c][:, i : i + 2, :].rearrange("p b k -> p (b k)").bitcast(FP8),
+                    in1=scale2[:].rearrange("p c k -> p (c k)"),
+                    op=ALU.mult,
+                )
+
+        def transp(j):
+            xg = xg_pool.tile([P, 2 * K], BF16, name="xg", align_bytes=64)
+            xg_of[j] = xg
+            words = xs_of[j][:].bitcast(F32)
+            dst = xg[:].bitcast(F32).rearrange("p (a g r u) -> p a g r u", a=2, g=2, u=2)
+            tps = [transposes(words, 512 * a) for a in range(2)]
+            for a in range(2):
+                nc.scalar.copy(
+                    out=dst[:, a], in_=tps[a][:].rearrange("p (g u) r -> p g r u", u=2)
+                )
+
+        def quant(j):
+            xc = xq_pool.tile([P, 512], U32, name="xc", align_bytes=64)
+            xsc = xq_pool.tile([P, 512], U8, name="xsc", align_bytes=64)
+            xq_of[j] = (xc, xsc)
+            nc.vector.quantize_mx(out=xc[:].bitcast(FP8X4), scales=xsc[:], in_=xg_of[j][:])
+
+        bias_f32 = const.tile([P, 512], F32, name="bias_f32")
+        q_of = {}
+
+        def mm_group(j, s):
+            a, h = divmod(s, 2)
+            xc, xsc = xq_of[j]
+            acc = psum_a.tile([P, 512], F32, name="acc")
+            acc_of[(j, s)] = acc
+            for g in range(2):
+                c0 = (2 * a + g) * P
+                nc.tensor.matmul_mx(
+                    out=acc[:],
+                    lhsT=xc[:, c0 : c0 + P].bitcast(FP8X4),
+                    lhsT_scale=xsc[:, c0 : c0 + P],
+                    rhs=wc[h][:, g * 512 : (g + 1) * 512].bitcast(FP8X4),
+                    rhs_scale=wsc[h][:, g * 512 : (g + 1) * 512],
+                    start=(g == 0),
+                    stop=(g == 1),
+                )
+
+        def q_tile(j, a):
+            if (j, a) not in q_of:
+                if a == 0:
+                    qa = q_pool.tile([P, D], F32, name="qa")
+                    q_of[(j, a)] = qa
+                else:
+                    qb = q_pool.tile([P, D], F32, name="qb")
+                    q_of[(j, a)] = qb
+            return q_of[(j, a)]
+
+        def evac(j):
+            q = q_tile(j, 0)
+            nc.scalar.copy(out=q[:, 0:512], in_=acc_of[(j, 0)][:])
+
+        def gadd(j):
+            q = q_tile(j, 0)
+            nc.gpsimd.tensor_tensor(out=q[:, 0:512], in0=q[:, 0:512], in1=bias_f32[:], op=ALU.add)
+
+        def bias_out(j, s):
+            a, h = divmod(s, 2)
+            q = q_tile(j, a)
+            nc.vector.tensor_tensor(
+                out=q[:, h * 512 : (h + 1) * 512],
+                in0=acc_of[(j, s)][:],
+                in1=bias_bc[:, h * 512 : (h + 1) * 512],
+                op=ALU.add,
+            )
+
+        def square(j, a):
+            i = 2 * j + a
+            junk = junk_pool.tile([P, D], BF16, name="junk")
+            nc.scalar.activation(
+                out=junk[:], in_=q_tile(j, a)[:], func=ACT.Square, accum_out=r2_all[:, i : i + 1]
+            )
+
+        def store(j, a):
+            nc.sync.dma_start(out=out_0[2 * j + a], in_=q_tile(j, a)[:])
+
+        widen(0)
+        for c in range(4):
+            wprep(c)
+        widen(1)
+        transp(0)
+        widen(2)
+        quant_w(0)
+        for c in range(4, 8):
+            wprep(c)
+        quant(0)
+        transp(1)
+        widen(3)
+        widen(4)
+        quant_w(1)
+        quant(1)
+        widen(5)
+        transp(2)
+        transp(3)
+        nc.scalar.copy(out=bias_f32[:], in_=bias_bc[:, 0:512])
+        for s in range(4):
+            mm_group(0, s)
+        transp(4)
+
+        for c in range(PAIRS):
+            more = c + 1 < PAIRS
+            if c + D_QUANT < PAIRS:
+                quant(c + D_QUANT)
+            if c + D_WIDEN < PAIRS:
+                widen(c + D_WIDEN)
+            if c < G_PAIRS:
+                evac(c)
+                if c > 0:
+                    square(c - 1, 1)
+                if more:
+                    mm_group(c + 1, 0)
+                if c + D_TRANSP < PAIRS:
+                    transp(c + D_TRANSP)
+                gadd(c)
+            else:
+                square(c - 1, 1)
+                if c + D_TRANSP < PAIRS:
+                    transp(c + D_TRANSP)
+                bias_out(c, 0)
+                if more:
+                    mm_group(c + 1, 0)
+            for s in range(1, 4):
+                bias_out(c, s)
+                if more:
+                    mm_group(c + 1, s)
+                if s % 2 == 1:
+                    store(c, s // 2)
+            square(c, 0)
+        square(PAIRS - 1, 1)
+
+        rt = psum_t.tile([P, 4, P], F32, name="tp")
+        x2 = rt[:, 0, :]
+        nc.tensor.transpose(x2, r2_all[:], ident[:])
+        y0 = const.tile([P, P], F32, name="y0")
+        nc.scalar.activation(out=y0[:], in_=x2, func=ACT.Sqrt)
+        nc.scalar.activation(out=warm[:, 1:2], in_=one_col[:], func=ACT.Exp)
+        rc = const.tile([P, P], F32, name="rc")
+        nc.vector.reciprocal(out=rc[:], in_=y0[:])
+        t1 = const.tile([P, P], F32, name="t1")
+        nc.vector.tensor_tensor(out=t1[:], in0=x2, in1=rc[:], op=ALU.mult)
+        s2 = const.tile([P, P], F32, name="s2")
+        nc.vector.tensor_tensor(out=s2[:], in0=t1[:], in1=y0[:], op=ALU.add)
+        mx = const.tile([P, 1], F32, name="mx")
+        nc.vector.reduce_max(out=mx[:], in_=s2[:], axis=AX.X)
+        nmx = const.tile([P, 1], F32, name="nmx")
+        nc.vector.tensor_scalar(out=nmx[:], in0=mx[:], scalar1=-0.5, scalar2=None, op0=ALU.mult)
+        ex = const.tile([P, P], F32, name="ex")
+        sm = const.tile([P, 1], F32, name="sm")
+        nc.scalar.activation(
+            out=ex[:], in_=s2[:], func=ACT.Exp, bias=nmx[:], scale=0.5, accum_out=sm[:]
+        )
+        rs = const.tile([P, 1], F32, name="rs")
+        nc.vector.reciprocal(out=rs[:], in_=sm[:])
+        wts = const.tile([P, P], F32, name="wts")
+        nc.vector.tensor_scalar(out=wts[:], in0=ex[:], scalar1=rs[:], scalar2=None, op0=ALU.mult)
+        nc.sync.dma_start(out=out_1[:, :], in_=wts[0:B, :])

@@ -23,6 +23,8 @@ G_PAIRS = 10
 D_WIDEN = 6
 D_TRANSP = 5
 D_QUANT = 2
+LAST_WIDEN_ROUND = PAIRS - D_WIDEN - 1
+ROOT_ROUNDS = (12, 15)
 
 
 def tile_candidateaware_clickednewsattention_pa_t_kernel(
@@ -33,7 +35,7 @@ def tile_candidateaware_clickednewsattention_pa_t_kernel(
         const = ctx.enter_context(tc.tile_pool(name="const", bufs=1))
         xs_pool = ctx.enter_context(tc.tile_pool(name="xs_pool", bufs=6))
         xg_pool = ctx.enter_context(tc.tile_pool(name="xg_pool", bufs=4))
-        xq_pool = ctx.enter_context(tc.tile_pool(name="xq_pool", bufs=3))
+        xq_pool = ctx.enter_context(tc.tile_pool(name="xq_pool", bufs=5))
         q_pool = ctx.enter_context(tc.tile_pool(name="q_pool", bufs=3))
         junk_pool = ctx.enter_context(tc.tile_pool(name="junk_pool", bufs=2))
         psum_t = ctx.enter_context(tc.psum_pool(name="psum_t", bufs=4))
@@ -87,10 +89,13 @@ def tile_candidateaware_clickednewsattention_pa_t_kernel(
         masks.make_identity(nc, ident[:])
         one_col = const.tile([P, 1], F32, name="one_col")
         nc.vector.memset(one_col[:], 1.0)
-        r2_all = const.tile([P, P], F32, name="r2_all")
-        nc.vector.memset(r2_all[:], 1.0)
-        warm = const.tile([P, 2], F32, name="warm")
-        nc.scalar.activation(out=warm[:, 0:1], in_=one_col[:], func=ACT.Sqrt)
+        r2_all = const.tile([P, B], F32, name="r2_all")
+        r_all = const.tile([P, P], F32, name="r_all")
+        nc.vector.memset(r_all[:], 1.0)
+        half = const.tile([P, B], F32, name="half")
+        nc.vector.memset(half[:], 0.5)
+        warm = const.tile([P, 1], F32, name="warm")
+        nc.scalar.activation(out=warm[:], in_=one_col[:], func=ACT.Exp)
         nc.scalar.copy(out=scale2[:, 1, :], in_=scale2[:, 0, :])
 
         wgrp = []
@@ -224,6 +229,11 @@ def tile_candidateaware_clickednewsattention_pa_t_kernel(
                 out=junk[:], in_=q_tile(j, a)[:], func=ACT.Square, accum_out=r2_all[:, i : i + 1]
             )
 
+        def roots(lo, hi):
+            nc.gpsimd.tensor_tensor(
+                out=r_all[:, lo:hi], in0=r2_all[:, lo:hi], in1=half[:, 0 : hi - lo], op=ALU.pow
+            )
+
         def store(j, a):
             nc.sync.dma_start(out=out_0[2 * j + a], in_=q_tile(j, a)[:])
 
@@ -250,12 +260,16 @@ def tile_candidateaware_clickednewsattention_pa_t_kernel(
             mm_group(0, s)
         transp(4)
 
+        rooted = 0
         for c in range(PAIRS):
             more = c + 1 < PAIRS
-            if c + D_QUANT < PAIRS:
-                quant(c + D_QUANT)
             if c + D_WIDEN < PAIRS:
+                quant(c + D_QUANT)
                 widen(c + D_WIDEN)
+            else:
+                first = LAST_WIDEN_ROUND + 1 + D_QUANT + 2 * (c - LAST_WIDEN_ROUND - 1)
+                for j in range(first, min(first + 2, PAIRS)):
+                    quant(j)
             if c < G_PAIRS:
                 evac(c)
                 if c > 0:
@@ -267,6 +281,9 @@ def tile_candidateaware_clickednewsattention_pa_t_kernel(
                 gadd(c)
             else:
                 square(c - 1, 1)
+                if c in ROOT_ROUNDS:
+                    roots(rooted, 2 * c)
+                    rooted = 2 * c
                 if c + D_TRANSP < PAIRS:
                     transp(c + D_TRANSP)
                 bias_out(c, 0)
@@ -279,28 +296,19 @@ def tile_candidateaware_clickednewsattention_pa_t_kernel(
                 if s % 2 == 1:
                     store(c, s // 2)
             square(c, 0)
+        roots(rooted, B - 1)
         square(PAIRS - 1, 1)
+        roots(B - 1, B)
 
         rt = psum_t.tile([P, 4, P], F32, name="tp")
-        x2 = rt[:, 0, :]
-        nc.tensor.transpose(x2, r2_all[:], ident[:])
-        y0 = const.tile([P, P], F32, name="y0")
-        nc.scalar.activation(out=y0[:], in_=x2, func=ACT.Sqrt)
-        nc.scalar.activation(out=warm[:, 1:2], in_=one_col[:], func=ACT.Exp)
-        rc = const.tile([P, P], F32, name="rc")
-        nc.vector.reciprocal(out=rc[:], in_=y0[:])
-        t1 = const.tile([P, P], F32, name="t1")
-        nc.vector.tensor_tensor(out=t1[:], in0=x2, in1=rc[:], op=ALU.mult)
-        s2 = const.tile([P, P], F32, name="s2")
-        nc.vector.tensor_tensor(out=s2[:], in0=t1[:], in1=y0[:], op=ALU.add)
-        mx = const.tile([P, 1], F32, name="mx")
-        nc.vector.reduce_max(out=mx[:], in_=s2[:], axis=AX.X)
+        rT = rt[:, 0, :]
+        nc.tensor.transpose(rT, r_all[:], ident[:])
         nmx = const.tile([P, 1], F32, name="nmx")
-        nc.vector.tensor_scalar(out=nmx[:], in0=mx[:], scalar1=-0.5, scalar2=None, op0=ALU.mult)
+        nc.vector.reduce_max(out=nmx[:], in_=rT, axis=AX.X, negate=True)
         ex = const.tile([P, P], F32, name="ex")
         sm = const.tile([P, 1], F32, name="sm")
         nc.scalar.activation(
-            out=ex[:], in_=s2[:], func=ACT.Exp, bias=nmx[:], scale=0.5, accum_out=sm[:]
+            out=ex[:], in_=rT, func=ACT.Exp, bias=nmx[:], scale=1.0, accum_out=sm[:]
         )
         rs = const.tile([P, 1], F32, name="rs")
         nc.vector.reciprocal(out=rs[:], in_=sm[:])

@@ -19,10 +19,11 @@ FLOPS = 2 * B * N * K * D
 
 PAIRS = B // 2
 CHUNKS = (2, 2, 4, 8, 8, 8)
-G_PAIRS = 10
-D_WIDEN = 6
-D_TRANSP = 5
+G_PAIRS = 11
+D_WIDEN = 5
+D_TRANSP = 4
 D_QUANT = 2
+N_DUMMY = 16
 LAST_WIDEN_ROUND = PAIRS - D_WIDEN - 1
 ROOT_ROUNDS = (12, 15)
 
@@ -84,6 +85,12 @@ def tile_candidateaware_clickednewsattention_pa_t_kernel(
         nc.sync.dma_start(out=bias_bc[:], in_=bq.partition_broadcast(P))
         load_x(4)
         load_x(5)
+
+        ones_bf = const.tile([P, 512], BF16, name="ones_bf")
+        nc.gpsimd.memset(ones_bf[:], 1.0)
+        dummy = psum_a.tile([P, 512], F32, name="acc")
+        for i in range(N_DUMMY):
+            nc.tensor.matmul(dummy[:], lhsT=ones_bf[:, 0:P], rhs=ones_bf[:], start=True, stop=True)
 
         ident = const.tile([P, P], F32, name="ident")
         masks.make_identity(nc, ident[:])
@@ -252,13 +259,11 @@ def tile_candidateaware_clickednewsattention_pa_t_kernel(
         widen(4)
         quant_w(1)
         quant(1)
-        widen(5)
         transp(2)
         transp(3)
         nc.scalar.copy(out=bias_f32[:], in_=bias_bc[:, 0:512])
         for s in range(4):
             mm_group(0, s)
-        transp(4)
 
         rooted = 0
         for c in range(PAIRS):

@@ -89,8 +89,12 @@ def tile_candidateaware_clickednewsattention_pa_t_kernel(
         ones_bf = const.tile([P, 512], BF16, name="ones_bf")
         nc.gpsimd.memset(ones_bf[:], 1.0)
         dummy = psum_a.tile([P, 512], F32, name="acc")
-        for i in range(N_DUMMY):
+
+        def dummy_matmul():
             nc.tensor.matmul(dummy[:], lhsT=ones_bf[:, 0:P], rhs=ones_bf[:], start=True, stop=True)
+
+        for i in range(N_DUMMY):
+            dummy_matmul()
 
         ident = const.tile([P, P], F32, name="ident")
         masks.make_identity(nc, ident[:])
@@ -116,12 +120,16 @@ def tile_candidateaware_clickednewsattention_pa_t_kernel(
             t = const.tile([P, K], U8, name="wsc%d" % h, align_bytes=64)
             wsc.append(t)
 
+        keep_warm = [True]
+
         def transposes(words, base):
             tp = psum_t.tile([P, 4, P], F32, name="tp")
             for s in range(4):
                 g, u = divmod(s, 2)
                 lo = base + 256 * g
                 nc.tensor.transpose(tp[:, s, :], words[:, lo + u : lo + 256 : 2], ident[:])
+            if keep_warm[0]:
+                dummy_matmul()
             return tp
 
         def wprep(c):
@@ -262,6 +270,7 @@ def tile_candidateaware_clickednewsattention_pa_t_kernel(
         transp(2)
         transp(3)
         nc.scalar.copy(out=bias_f32[:], in_=bias_bc[:, 0:512])
+        keep_warm[0] = False
         for s in range(4):
             mm_group(0, s)
 

@@ -25,7 +25,7 @@ D_TRANSP = 4
 D_QUANT = 2
 N_DUMMY = 16
 LAST_WIDEN_ROUND = PAIRS - D_WIDEN - 1
-ROOT_ROUNDS = (12, 15)
+ROOT_ROUNDS = (12, 14, 15)
 
 
 def tile_candidateaware_clickednewsattention_pa_t_kernel(
@@ -34,11 +34,11 @@ def tile_candidateaware_clickednewsattention_pa_t_kernel(
     nc = tc.nc
     with ExitStack() as ctx:
         const = ctx.enter_context(tc.tile_pool(name="const", bufs=1))
-        xs_pool = ctx.enter_context(tc.tile_pool(name="xs_pool", bufs=6))
-        xg_pool = ctx.enter_context(tc.tile_pool(name="xg_pool", bufs=4))
+        xs_pool = ctx.enter_context(tc.tile_pool(name="xs_pool", bufs=7))
+        xg_pool = ctx.enter_context(tc.tile_pool(name="xg_pool", bufs=6))
         xq_pool = ctx.enter_context(tc.tile_pool(name="xq_pool", bufs=5))
-        q_pool = ctx.enter_context(tc.tile_pool(name="q_pool", bufs=3))
-        junk_pool = ctx.enter_context(tc.tile_pool(name="junk_pool", bufs=2))
+        q_pool = ctx.enter_context(tc.tile_pool(name="q_pool", bufs=5))
+        junk_pool = ctx.enter_context(tc.tile_pool(name="junk_pool", bufs=3))
         psum_t = ctx.enter_context(tc.psum_pool(name="psum_t", bufs=4))
         psum_a = ctx.enter_context(tc.psum_pool(name="psum_a", bufs=4))
         ctx.enter_context(tc.manual_schedule())
@@ -311,7 +311,26 @@ def tile_candidateaware_clickednewsattention_pa_t_kernel(
                     store(c, s // 2)
             square(c, 0)
         roots(rooted, B - 1)
-        square(PAIRS - 1, 1)
+        q_last = q_tile(PAIRS - 1, 1)
+        junk = junk_pool.tile([P, D], BF16, name="junk")
+        part = const.tile([P, 2], F32, name="part")
+        nc.scalar.activation(
+            out=junk[:, 0:512], in_=q_last[:, 0:512], func=ACT.Square, accum_out=part[:, 0:1]
+        )
+        junk_v = const.tile([P, 512], BF16, name="junk_v")
+        part_v = const.tile([P, 1], F32, name="part_v")
+        nc.vector.scalar_tensor_tensor(
+            out=junk_v[:],
+            in0=q_last[:, 512:D],
+            scalar=1.0,
+            in1=q_last[:, 512:D],
+            op0=ALU.mult,
+            op1=ALU.mult,
+            accum_out=part_v[:],
+        )
+        nc.vector.tensor_tensor(
+            out=r2_all[:, B - 1 : B], in0=part[:, 0:1], in1=part_v[:], op=ALU.add
+        )
         roots(B - 1, B)
 
         rt = psum_t.tile([P, 4, P], F32, name="tp")

@@ -23,7 +23,6 @@ G_PAIRS = 11
 D_WIDEN = 5
 D_TRANSP = 4
 D_QUANT = 2
-N_DUMMY = 16
 LAST_WIDEN_ROUND = PAIRS - D_WIDEN - 1
 ROOT_ROUNDS = (12, 14, 15)
 
@@ -86,16 +85,6 @@ def tile_candidateaware_clickednewsattention_pa_t_kernel(
         load_x(4)
         load_x(5)
 
-        ones_bf = const.tile([P, 512], BF16, name="ones_bf")
-        nc.gpsimd.memset(ones_bf[:], 1.0)
-        dummy = psum_a.tile([P, 512], F32, name="acc")
-
-        def dummy_matmul():
-            nc.tensor.matmul(dummy[:], lhsT=ones_bf[:, 0:P], rhs=ones_bf[:], start=True, stop=True)
-
-        for i in range(N_DUMMY):
-            dummy_matmul()
-
         ident = const.tile([P, P], F32, name="ident")
         masks.make_identity(nc, ident[:])
         one_col = const.tile([P, 1], F32, name="one_col")
@@ -120,16 +109,12 @@ def tile_candidateaware_clickednewsattention_pa_t_kernel(
             t = const.tile([P, K], U8, name="wsc%d" % h, align_bytes=64)
             wsc.append(t)
 
-        keep_warm = [True]
-
         def transposes(words, base):
             tp = psum_t.tile([P, 4, P], F32, name="tp")
             for s in range(4):
                 g, u = divmod(s, 2)
                 lo = base + 256 * g
                 nc.tensor.transpose(tp[:, s, :], words[:, lo + u : lo + 256 : 2], ident[:])
-            if keep_warm[0]:
-                dummy_matmul()
             return tp
 
         def wprep(c):
@@ -270,7 +255,6 @@ def tile_candidateaware_clickednewsattention_pa_t_kernel(
         transp(2)
         transp(3)
         nc.scalar.copy(out=bias_f32[:], in_=bias_bc[:, 0:512])
-        keep_warm[0] = False
         for s in range(4):
             mm_group(0, s)
 

@@ -18,7 +18,7 @@ P = 128
 FLOPS = 2 * B * N * K * D
 
 PAIRS = B // 2
-CHUNKS = (2, 2, 4, 8, 8, 8)
+CHUNKS = (2, 2, 4, 8, 16)
 G_PAIRS = 11
 D_WIDEN = 5
 D_TRANSP = 4
@@ -74,16 +74,15 @@ def tile_candidateaware_clickednewsattention_pa_t_kernel(
             )
 
         load_x(0)
+        load_x(1)
         load_w(0)
         load_w(1)
-        load_x(1)
         load_x(2)
         load_w(2)
         load_w(3)
         load_x(3)
         nc.sync.dma_start(out=bias_bc[:], in_=bq.partition_broadcast(P))
         load_x(4)
-        load_x(5)
 
         ident = const.tile([P, P], F32, name="ident")
         masks.make_identity(nc, ident[:])
@@ -272,10 +271,10 @@ def tile_candidateaware_clickednewsattention_pa_t_kernel(
                 evac(c)
                 if c > 0:
                     square(c - 1, 1)
-                if more:
-                    mm_group(c + 1, 0)
                 if c + D_TRANSP < PAIRS:
                     transp(c + D_TRANSP)
+                if more:
+                    mm_group(c + 1, 0)
                 gadd(c)
             else:
                 square(c - 1, 1)

@@ -20,6 +20,8 @@ FLOPS = 2 * B * N * K * D
 PAIRS = B // 2
 CHUNKS = (2, 2, 4, 8, 16)
 G_PAIRS = 11
+G_EXTRA = 128
+G_COLS = 512 + G_EXTRA
 D_WIDEN = 5
 D_TRANSP = 4
 D_QUANT = 2
@@ -173,7 +175,7 @@ def tile_candidateaware_clickednewsattention_pa_t_kernel(
             xq_of[j] = (xc, xsc)
             nc.vector.quantize_mx(out=xc[:].bitcast(FP8X4), scales=xsc[:], in_=xg_of[j][:])
 
-        bias_f32 = const.tile([P, 512], F32, name="bias_f32")
+        bias_f32 = const.tile([P, G_COLS], F32, name="bias_f32")
         q_of = {}
 
         def mm_group(j, s):
@@ -206,18 +208,20 @@ def tile_candidateaware_clickednewsattention_pa_t_kernel(
         def evac(j):
             q = q_tile(j, 0)
             nc.scalar.copy(out=q[:, 0:512], in_=acc_of[(j, 0)][:])
+            nc.scalar.copy(out=q[:, 512:G_COLS], in_=acc_of[(j, 1)][:, 0:G_EXTRA])
 
         def gadd(j):
             q = q_tile(j, 0)
-            nc.gpsimd.tensor_tensor(out=q[:, 0:512], in0=q[:, 0:512], in1=bias_f32[:], op=ALU.add)
+            nc.gpsimd.tensor_tensor(out=q[:, 0:G_COLS], in0=q[:, 0:G_COLS], in1=bias_f32[:], op=ALU.add)
 
         def bias_out(j, s):
             a, h = divmod(s, 2)
             q = q_tile(j, a)
+            lo = G_EXTRA if (s == 1 and j < G_PAIRS) else 0
             nc.vector.tensor_tensor(
-                out=q[:, h * 512 : (h + 1) * 512],
-                in0=acc_of[(j, s)][:],
-                in1=bias_bc[:, h * 512 : (h + 1) * 512],
+                out=q[:, h * 512 + lo : (h + 1) * 512],
+                in0=acc_of[(j, s)][:, lo:512],
+                in1=bias_bc[:, h * 512 + lo : (h + 1) * 512],
                 op=ALU.add,
             )
 
@@ -253,7 +257,7 @@ def tile_candidateaware_clickednewsattention_pa_t_kernel(
         quant(1)
         transp(2)
         transp(3)
-        nc.scalar.copy(out=bias_f32[:], in_=bias_bc[:, 0:512])
+        nc.scalar.copy(out=bias_f32[:], in_=bias_bc[:, 0:G_COLS])
         for s in range(4):
             mm_group(0, s)
 

@@ -146,15 +146,15 @@ def tile_candidateaware_clickednewsattention_pa_t_kernel(
                 for a in range(2):
                     nc.vector.tensor_tensor(
                         out=xs[:, a * K : (a + 1) * K],
-                        in0=xbytes[c][:, i + a, :].bitcast(FP8),
-                        in1=scale2[:, 0, :],
+                        in0=scale2[:, 0, :],
+                        in1=xbytes[c][:, i + a, :].bitcast(FP8),
                         op=ALU.mult,
                     )
             else:
                 nc.vector.tensor_tensor(
                     out=xs[:],
-                    in0=xbytes[c][:, i : i + 2, :].rearrange("p b k -> p (b k)").bitcast(FP8),
-                    in1=scale2[:].rearrange("p c k -> p (c k)"),
+                    in0=scale2[:].rearrange("p c k -> p (c k)"),
+                    in1=xbytes[c][:, i : i + 2, :].rearrange("p b k -> p (b k)").bitcast(FP8),
                     op=ALU.mult,
                 )
 

@@ -17,15 +17,15 @@ B, N, K, D = 32, 128, 1024, 1024
 P = 128
 FLOPS = 2 * B * N * K * D
 
+TUNE = False
 PAIRS = B // 2
 CHUNKS = (2, 2, 4, 8, 16)
-G_PAIRS = 11
-G_EXTRA = 128
-G_COLS = 512 + G_EXTRA
-D_WIDEN = 5
-D_TRANSP = 4
+N_WIDE = 4
+D_EXIT = 4
+D_TNEW = 5
 D_QUANT = 2
-LAST_WIDEN_ROUND = PAIRS - D_WIDEN - 1
+D_CAST = 6
+LAST_EXIT_ROUND = PAIRS - D_EXIT - 1
 ROOT_ROUNDS = (12, 14, 15)
 
 
@@ -35,13 +35,14 @@ def tile_candidateaware_clickednewsattention_pa_t_kernel(
     nc = tc.nc
     with ExitStack() as ctx:
         const = ctx.enter_context(tc.tile_pool(name="const", bufs=1))
-        xs_pool = ctx.enter_context(tc.tile_pool(name="xs_pool", bufs=7))
+        xs_pool = ctx.enter_context(tc.tile_pool(name="xs_pool", bufs=10))
         xg_pool = ctx.enter_context(tc.tile_pool(name="xg_pool", bufs=6))
         xq_pool = ctx.enter_context(tc.tile_pool(name="xq_pool", bufs=5))
         q_pool = ctx.enter_context(tc.tile_pool(name="q_pool", bufs=5))
         junk_pool = ctx.enter_context(tc.tile_pool(name="junk_pool", bufs=3))
         psum_t = ctx.enter_context(tc.psum_pool(name="psum_t", bufs=4))
         psum_a = ctx.enter_context(tc.psum_pool(name="psum_a", bufs=4))
+        xr_pool = ctx.enter_context(tc.tile_pool(name="xr_pool", bufs=3))
         ctx.enter_context(tc.manual_schedule())
 
         scale2 = const.tile([P, 2, K], F32, name="scale2")
@@ -61,6 +62,7 @@ def tile_candidateaware_clickednewsattention_pa_t_kernel(
             t = const.tile([P, 2, K], BF16, name="wraw%d" % c)
             wraw.append(t)
         bias_bc = const.tile([P, D], BF16, name="bias_bc")
+        sc8 = const.tile([P, 8], F32, name="sc8")
 
         def load_x(c):
             b0 = sum(CHUNKS[:c])
@@ -77,6 +79,10 @@ def tile_candidateaware_clickednewsattention_pa_t_kernel(
 
         load_x(0)
         load_x(1)
+        nc.sync.dma_start(
+            out=sc8[:].rearrange("p (g t) -> p g t", t=4),
+            in_=cand_topics_scale.rearrange("a b (g p t) -> p (a b g) t", g=2, p=P, t=4),
+        )
         load_w(0)
         load_w(1)
         load_x(2)
@@ -98,6 +104,12 @@ def tile_candidateaware_clickednewsattention_pa_t_kernel(
         warm = const.tile([P, 1], F32, name="warm")
         nc.scalar.activation(out=warm[:], in_=one_col[:], func=ACT.Exp)
         nc.scalar.copy(out=scale2[:, 1, :], in_=scale2[:, 0, :])
+        gate_junk = const.tile([P, 2], U32, name="gate_junk")
+        sck = const.tile([P, K], F32, name="sck")
+        nc.scalar.copy(
+            out=sck[:].rearrange("p (g r t) -> p g r t", g=2, t=4),
+            in_=sc8[:].rearrange("p (g t) -> p g t", t=4).unsqueeze(2).to_broadcast([P, 2, P, 4]),
+        )
 
         wgrp = []
         wc = []
@@ -137,6 +149,7 @@ def tile_candidateaware_clickednewsattention_pa_t_kernel(
         xg_of = {}
         xq_of = {}
         acc_of = {}
+        tp_of = {}
 
         def widen(j):
             xs = xs_pool.tile([P, 2 * K], BF16, name="xs", align_bytes=64)
@@ -169,13 +182,86 @@ def tile_candidateaware_clickednewsattention_pa_t_kernel(
                     out=dst[:, a], in_=tps[a][:].rearrange("p (g u) r -> p g r u", u=2)
                 )
 
+        whole_cast = {}
+
+        def cast_pair(j):
+            xs = xs_pool.tile([P, 2 * K], BF16, name="xs", align_bytes=64)
+            xs_of[j] = xs
+            whole_cast[j] = True
+            c, i = where[2 * j]
+            if TUNE:
+                nc.scalar.copy(out=xs[:, 0:K], in_=xbytes[c][:, i, :].bitcast(FP8))
+            else:
+                nc.scalar.copy(
+                    out=xs[:],
+                    in_=xbytes[c][:, i : i + 2, :].rearrange("p b k -> p (b k)").bitcast(FP8),
+                )
+
+        def cast_user(j, a):
+            if a == 0:
+                xs = xs_pool.tile([P, 2 * K], BF16, name="xs", align_bytes=64)
+                xs_of[j] = xs
+                whole_cast[j] = False
+            c, i = where[2 * j + a]
+            w = K // 2 if TUNE else K
+            nc.scalar.copy(
+                out=xs_of[j][:, a * K : a * K + w], in_=xbytes[c][:, i, 0:w].bitcast(FP8)
+            )
+
+        def t_new(j):
+            words = xs_of[j][:].bitcast(F32)
+            tps = []
+            for a in range(2):
+                tp = psum_t.tile([P, 4, P], F32, name="tp")
+                for s in range(4):
+                    if a == 0:
+                        g, u = divmod(s, 2)
+                    else:
+                        u, g = divmod(s, 2)
+                    lo = 512 * a + 256 * g
+                    if TUNE:
+                        lo = 256 * g if whole_cast[j] else 512 * a
+                    nc.tensor.transpose(tp[:, s, :], words[:, lo + u : lo + 256 : 2], ident[:])
+                tps.append(tp)
+            tp_of[j] = tps
+
+        xr_of = {}
+
+        def copy0(j):
+            xr = xr_pool.tile([P, K], BF16, name="xr", align_bytes=64)
+            xr_of[j] = xr
+            nc.scalar.copy(
+                out=xr[:].bitcast(F32).rearrange("p (g r u) -> p g r u", g=2, u=2),
+                in_=tp_of[j][0][:].rearrange("p (g u) r -> p g r u", u=2),
+            )
+
+        def exit1(j):
+            xg = xg_pool.tile([P, 2 * K], BF16, name="xg", align_bytes=64)
+            xg_of[j] = xg
+            nc.vector.tensor_tensor(
+                out=xg[:, K : 2 * K].rearrange("p (m u e) -> p m u e", u=2, e=2),
+                in0=tp_of[j][1][:]
+                .rearrange("p s r -> p (s r)")
+                .bitcast(BF16)
+                .rearrange("p (u m e) -> p m u e", u=2, e=2),
+                in1=sck[:].rearrange("p (m u e) -> p m u e", u=2, e=2),
+                op=ALU.mult,
+            )
+
+        def gmul(j):
+            nc.gpsimd.tensor_tensor(
+                out=xg_of[j][:, 0:K], in0=xr_of[j][:], in1=sck[:], op=ALU.mult
+            )
+
         def quant(j):
             xc = xq_pool.tile([P, 512], U32, name="xc", align_bytes=64)
             xsc = xq_pool.tile([P, 512], U8, name="xsc", align_bytes=64)
             xq_of[j] = (xc, xsc)
             nc.vector.quantize_mx(out=xc[:].bitcast(FP8X4), scales=xsc[:], in_=xg_of[j][:])
 
-        bias_f32 = const.tile([P, G_COLS], F32, name="bias_f32")
+        def gate(j):
+            nc.gpsimd.tensor_copy(out=gate_junk[:], in_=xq_of[j][0][:, 0:2])
+
         q_of = {}
 
         def mm_group(j, s):
@@ -205,23 +291,13 @@ def tile_candidateaware_clickednewsattention_pa_t_kernel(
                     q_of[(j, a)] = qb
             return q_of[(j, a)]
 
-        def evac(j):
-            q = q_tile(j, 0)
-            nc.scalar.copy(out=q[:, 0:512], in_=acc_of[(j, 0)][:])
-            nc.scalar.copy(out=q[:, 512:G_COLS], in_=acc_of[(j, 1)][:, 0:G_EXTRA])
-
-        def gadd(j):
-            q = q_tile(j, 0)
-            nc.gpsimd.tensor_tensor(out=q[:, 0:G_COLS], in0=q[:, 0:G_COLS], in1=bias_f32[:], op=ALU.add)
-
         def bias_out(j, s):
             a, h = divmod(s, 2)
             q = q_tile(j, a)
-            lo = G_EXTRA if (s == 1 and j < G_PAIRS) else 0
             nc.vector.tensor_tensor(
-                out=q[:, h * 512 + lo : (h + 1) * 512],
-                in0=acc_of[(j, s)][:, lo:512],
-                in1=bias_bc[:, h * 512 + lo : (h + 1) * 512],
+                out=q[:, h * 512 : (h + 1) * 512],
+                in0=acc_of[(j, s)][:],
+                in1=bias_bc[:, h * 512 : (h + 1) * 512],
                 op=ALU.add,
             )
 
@@ -249,48 +325,44 @@ def tile_candidateaware_clickednewsattention_pa_t_kernel(
         quant_w(0)
         for c in range(4, 8):
             wprep(c)
+        cast_pair(4)
         quant(0)
         transp(1)
         widen(3)
-        widen(4)
         quant_w(1)
         quant(1)
         transp(2)
-        transp(3)
-        nc.scalar.copy(out=bias_f32[:], in_=bias_bc[:, 0:G_COLS])
+        cast_pair(5)
+        t_new(4)
+        copy0(4)
         for s in range(4):
             mm_group(0, s)
 
         rooted = 0
         for c in range(PAIRS):
             more = c + 1 < PAIRS
-            if c + D_WIDEN < PAIRS:
+            if c <= LAST_EXIT_ROUND:
                 quant(c + D_QUANT)
-                widen(c + D_WIDEN)
+                gate(c + D_QUANT)
+                exit1(c + D_EXIT)
+                gmul(c + D_EXIT)
             else:
-                first = LAST_WIDEN_ROUND + 1 + D_QUANT + 2 * (c - LAST_WIDEN_ROUND - 1)
+                first = LAST_EXIT_ROUND + 1 + D_QUANT + 2 * (c - LAST_EXIT_ROUND - 1)
                 for j in range(first, min(first + 2, PAIRS)):
                     quant(j)
-            if c < G_PAIRS:
-                evac(c)
-                if c > 0:
-                    square(c - 1, 1)
-                if c + D_TRANSP < PAIRS:
-                    transp(c + D_TRANSP)
-                if more:
-                    mm_group(c + 1, 0)
-                gadd(c)
-            else:
+            if c > 0:
                 square(c - 1, 1)
-                if c in ROOT_ROUNDS:
-                    roots(rooted, 2 * c)
-                    rooted = 2 * c
-                if c + D_TRANSP < PAIRS:
-                    transp(c + D_TRANSP)
-                bias_out(c, 0)
-                if more:
-                    mm_group(c + 1, 0)
-            for s in range(1, 4):
+            if c in ROOT_ROUNDS:
+                roots(rooted, 2 * c)
+                rooted = 2 * c
+            if c + D_CAST < PAIRS:
+                cast_pair(c + D_CAST)
+            if c == 0:
+                transp(N_WIDE - 1)
+            if c + D_TNEW < PAIRS:
+                t_new(c + D_TNEW)
+                copy0(c + D_TNEW)
+            for s in range(4):
                 bias_out(c, s)
                 if more:
                     mm_group(c + 1, s)

@@ -45,6 +45,11 @@ def tile_candidateaware_clickednewsattention_pa_t_kernel(
         xr_pool = ctx.enter_context(tc.tile_pool(name="xr_pool", bufs=3))
         ctx.enter_context(tc.manual_schedule())
 
+        sc8 = const.tile([P, 8], F32, name="sc8")
+        nc.scalar.dma_start(
+            out=sc8[:].rearrange("p (g t) -> p g t", t=4),
+            in_=cand_topics_scale.rearrange("a b (g p t) -> p (a b g) t", g=2, p=P, t=4),
+        )
         scale2 = const.tile([P, 2, K], F32, name="scale2")
         nc.sync.dma_start(
             out=scale2[:, 0, :],
@@ -62,7 +67,6 @@ def tile_candidateaware_clickednewsattention_pa_t_kernel(
             t = const.tile([P, 2, K], BF16, name="wraw%d" % c)
             wraw.append(t)
         bias_bc = const.tile([P, D], BF16, name="bias_bc")
-        sc8 = const.tile([P, 8], F32, name="sc8")
 
         def load_x(c):
             b0 = sum(CHUNKS[:c])
@@ -79,10 +83,6 @@ def tile_candidateaware_clickednewsattention_pa_t_kernel(
 
         load_x(0)
         load_x(1)
-        nc.sync.dma_start(
-            out=sc8[:].rearrange("p (g t) -> p g t", t=4),
-            in_=cand_topics_scale.rearrange("a b (g p t) -> p (a b g) t", g=2, p=P, t=4),
-        )
         load_w(0)
         load_w(1)
         load_x(2)
@@ -103,13 +103,13 @@ def tile_candidateaware_clickednewsattention_pa_t_kernel(
         nc.vector.memset(half[:], 0.5)
         warm = const.tile([P, 1], F32, name="warm")
         nc.scalar.activation(out=warm[:], in_=one_col[:], func=ACT.Exp)
-        nc.scalar.copy(out=scale2[:, 1, :], in_=scale2[:, 0, :])
         gate_junk = const.tile([P, 2], U32, name="gate_junk")
         sck = const.tile([P, K], F32, name="sck")
         nc.scalar.copy(
             out=sck[:].rearrange("p (g r t) -> p g r t", g=2, t=4),
             in_=sc8[:].rearrange("p (g t) -> p g t", t=4).unsqueeze(2).to_broadcast([P, 2, P, 4]),
         )
+        nc.scalar.copy(out=scale2[:, 1, :], in_=scale2[:, 0, :])
 
         wgrp = []
         wc = []

@@ -19,7 +19,7 @@ FLOPS = 2 * B * N * K * D
 
 TUNE = False
 PAIRS = B // 2
-CHUNKS = (2, 2, 4, 8, 16)
+CHUNKS = (2, 2, 4, 2, 6, 16)
 N_WIDE = 4
 D_EXIT = 4
 D_TNEW = 5
@@ -86,11 +86,12 @@ def tile_candidateaware_clickednewsattention_pa_t_kernel(
         load_w(0)
         load_w(1)
         load_x(2)
+        load_x(3)
         load_w(2)
         load_w(3)
-        load_x(3)
-        nc.sync.dma_start(out=bias_bc[:], in_=bq.partition_broadcast(P))
         load_x(4)
+        nc.sync.dma_start(out=bias_bc[:], in_=bq.partition_broadcast(P))
+        load_x(5)
 
         ident = const.tile([P, P], F32, name="ident")
         masks.make_identity(nc, ident[:])
@@ -321,20 +322,20 @@ def tile_candidateaware_clickednewsattention_pa_t_kernel(
             wprep(c)
         widen(1)
         transp(0)
+        cast_pair(4)
         widen(2)
         quant_w(0)
         for c in range(4, 8):
             wprep(c)
-        cast_pair(4)
         quant(0)
         transp(1)
         widen(3)
         quant_w(1)
         quant(1)
         transp(2)
-        cast_pair(5)
         t_new(4)
         copy0(4)
+        cast_pair(5)
         for s in range(4):
             mm_group(0, s)
 

@@ -24,6 +24,8 @@ N_WIDE = 4
 D_EXIT = 4
 D_TNEW = 5
 D_QUANT = 2
+G_MORE = 64
+G_ROWS = G_MORE // 4
 D_CAST = 6
 LAST_EXIT_ROUND = PAIRS - D_EXIT - 1
 ROOT_ROUNDS = (12, 14, 15)
@@ -105,10 +107,14 @@ def tile_candidateaware_clickednewsattention_pa_t_kernel(
         warm = const.tile([P, 1], F32, name="warm")
         nc.scalar.activation(out=warm[:], in_=one_col[:], func=ACT.Exp)
         gate_junk = const.tile([P, 2], U32, name="gate_junk")
-        sck = const.tile([P, K], F32, name="sck")
+        sck = const.tile([P, K + G_MORE], F32, name="sck")
         nc.scalar.copy(
-            out=sck[:].rearrange("p (g r t) -> p g r t", g=2, t=4),
+            out=sck[:, 0:K].rearrange("p (g r t) -> p g r t", g=2, t=4),
             in_=sc8[:].rearrange("p (g t) -> p g t", t=4).unsqueeze(2).to_broadcast([P, 2, P, 4]),
+        )
+        nc.scalar.copy(
+            out=sck[:, K : K + G_MORE].rearrange("p (r t) -> p r t", t=4),
+            in_=sc8[:, 0:4].unsqueeze(1).to_broadcast([P, G_ROWS, 4]),
         )
         nc.scalar.copy(out=scale2[:, 1, :], in_=scale2[:, 0, :])
 
@@ -229,29 +235,33 @@ def tile_candidateaware_clickednewsattention_pa_t_kernel(
         xr_of = {}
 
         def copy0(j):
-            xr = xr_pool.tile([P, K], BF16, name="xr", align_bytes=64)
+            xr = xr_pool.tile([P, K + G_MORE], BF16, name="xr", align_bytes=64)
             xr_of[j] = xr
             nc.scalar.copy(
-                out=xr[:].bitcast(F32).rearrange("p (g r u) -> p g r u", g=2, u=2),
+                out=xr[:, 0:K].bitcast(F32).rearrange("p (g r u) -> p g r u", g=2, u=2),
                 in_=tp_of[j][0][:].rearrange("p (g u) r -> p g r u", u=2),
+            )
+            nc.scalar.copy(
+                out=xr[:, K : K + G_MORE].bitcast(F32).rearrange("p (r u) -> p r u", u=2),
+                in_=tp_of[j][1][:, 0:4:2, 0:G_ROWS].rearrange("p u r -> p r u"),
             )
 
         def exit1(j):
             xg = xg_pool.tile([P, 2 * K], BF16, name="xg", align_bytes=64)
             xg_of[j] = xg
             nc.vector.tensor_tensor(
-                out=xg[:, K : 2 * K].rearrange("p (m u e) -> p m u e", u=2, e=2),
+                out=xg[:, K + G_MORE : 2 * K].rearrange("p (m u e) -> p m u e", u=2, e=2),
                 in0=tp_of[j][1][:]
                 .rearrange("p s r -> p (s r)")
                 .bitcast(BF16)
-                .rearrange("p (u m e) -> p m u e", u=2, e=2),
-                in1=sck[:].rearrange("p (m u e) -> p m u e", u=2, e=2),
+                .rearrange("p (u m e) -> p m u e", u=2, e=2)[:, G_ROWS : 2 * P],
+                in1=sck[:, G_MORE:K].rearrange("p (m u e) -> p m u e", u=2, e=2),
                 op=ALU.mult,
             )
 
         def gmul(j):
             nc.gpsimd.tensor_tensor(
-                out=xg_of[j][:, 0:K], in0=xr_of[j][:], in1=sck[:], op=ALU.mult
+                out=xg_of[j][:, 0 : K + G_MORE], in0=xr_of[j][:], in1=sck[:], op=ALU.mult
             )
 
         def quant(j):

@@ -24,7 +24,7 @@ N_WIDE = 4
 D_EXIT = 4
 D_TNEW = 5
 D_QUANT = 2
-G_MORE = 64
+G_MORE = 128
 G_ROWS = G_MORE // 4
 D_CAST = 6
 LAST_EXIT_ROUND = PAIRS - D_EXIT - 1
@@ -38,7 +38,8 @@ def tile_candidateaware_clickednewsattention_pa_t_kernel(
     with ExitStack() as ctx:
         const = ctx.enter_context(tc.tile_pool(name="const", bufs=1))
         xs_pool = ctx.enter_context(tc.tile_pool(name="xs_pool", bufs=10))
-        xg_pool = ctx.enter_context(tc.tile_pool(name="xg_pool", bufs=6))
+        xg_head = ctx.enter_context(tc.tile_pool(name="xg_head", bufs=N_WIDE))
+        xg_pool = ctx.enter_context(tc.tile_pool(name="xg_pool", bufs=2))
         xq_pool = ctx.enter_context(tc.tile_pool(name="xq_pool", bufs=5))
         q_pool = ctx.enter_context(tc.tile_pool(name="q_pool", bufs=5))
         junk_pool = ctx.enter_context(tc.tile_pool(name="junk_pool", bufs=3))
@@ -179,7 +180,7 @@ def tile_candidateaware_clickednewsattention_pa_t_kernel(
                 )
 
         def transp(j):
-            xg = xg_pool.tile([P, 2 * K], BF16, name="xg", align_bytes=64)
+            xg = xg_head.tile([P, 2 * K], BF16, name="xg", align_bytes=64)
             xg_of[j] = xg
             words = xs_of[j][:].bitcast(F32)
             dst = xg[:].bitcast(F32).rearrange("p (a g r u) -> p a g r u", a=2, g=2, u=2)
@@ -246,9 +247,12 @@ def tile_candidateaware_clickednewsattention_pa_t_kernel(
                 in_=tp_of[j][1][:, 0:4:2, 0:G_ROWS].rearrange("p u r -> p r u"),
             )
 
-        def exit1(j):
+        def new_xg(j):
             xg = xg_pool.tile([P, 2 * K], BF16, name="xg", align_bytes=64)
             xg_of[j] = xg
+
+        def exit1(j):
+            xg = xg_of[j]
             nc.vector.tensor_tensor(
                 out=xg[:, K + G_MORE : 2 * K].rearrange("p (m u e) -> p m u e", u=2, e=2),
                 in0=tp_of[j][1][:]
@@ -354,8 +358,9 @@ def tile_candidateaware_clickednewsattention_pa_t_kernel(
             more = c + 1 < PAIRS
             if c <= LAST_EXIT_ROUND:
                 quant(c + D_QUANT)
-                gate(c + D_QUANT)
-                exit1(c + D_EXIT)
+                if c < 2:
+                    gate(c + D_QUANT)
+                new_xg(c + D_EXIT)
                 gmul(c + D_EXIT)
             else:
                 first = LAST_EXIT_ROUND + 1 + D_QUANT + 2 * (c - LAST_EXIT_ROUND - 1)
@@ -377,6 +382,8 @@ def tile_candidateaware_clickednewsattention_pa_t_kernel(
                 bias_out(c, s)
                 if more:
                     mm_group(c + 1, s)
+                if s == 0 and c <= LAST_EXIT_ROUND:
+                    exit1(c + D_EXIT)
                 if s % 2 == 1:
                     store(c, s // 2)
             square(c, 0)

@@ -38,7 +38,7 @@ def tile_candidateaware_clickednewsattention_pa_t_kernel(
     with ExitStack() as ctx:
         const = ctx.enter_context(tc.tile_pool(name="const", bufs=1))
         xs_pool = ctx.enter_context(tc.tile_pool(name="xs_pool", bufs=10))
-        xg_head = ctx.enter_context(tc.tile_pool(name="xg_head", bufs=N_WIDE))
+        xg_head = ctx.enter_context(tc.tile_pool(name="xg_head", bufs=2))
         xg_pool = ctx.enter_context(tc.tile_pool(name="xg_pool", bufs=2))
         xq_pool = ctx.enter_context(tc.tile_pool(name="xq_pool", bufs=5))
         q_pool = ctx.enter_context(tc.tile_pool(name="q_pool", bufs=5))
@@ -179,9 +179,16 @@ def tile_candidateaware_clickednewsattention_pa_t_kernel(
                     op=ALU.mult,
                 )
 
+        def new_xg(j):
+            if j < 2:
+                xg = xg_head.tile([P, 2 * K], BF16, name="xg", align_bytes=64)
+                xg_of[j] = xg
+            else:
+                xg = xg_pool.tile([P, 2 * K], BF16, name="xg", align_bytes=64)
+                xg_of[j] = xg
+
         def transp(j):
-            xg = xg_head.tile([P, 2 * K], BF16, name="xg", align_bytes=64)
-            xg_of[j] = xg
+            xg = xg_of[j]
             words = xs_of[j][:].bitcast(F32)
             dst = xg[:].bitcast(F32).rearrange("p (a g r u) -> p a g r u", a=2, g=2, u=2)
             tps = [transposes(words, 512 * a) for a in range(2)]
@@ -246,10 +253,6 @@ def tile_candidateaware_clickednewsattention_pa_t_kernel(
                 out=xr[:, K : K + G_MORE].bitcast(F32).rearrange("p (r u) -> p r u", u=2),
                 in_=tp_of[j][1][:, 0:4:2, 0:G_ROWS].rearrange("p u r -> p r u"),
             )
-
-        def new_xg(j):
-            xg = xg_pool.tile([P, 2 * K], BF16, name="xg", align_bytes=64)
-            xg_of[j] = xg
 
         def exit1(j):
             xg = xg_of[j]
@@ -335,6 +338,8 @@ def tile_candidateaware_clickednewsattention_pa_t_kernel(
         for c in range(4):
             wprep(c)
         widen(1)
+        for j in range(N_WIDE):
+            new_xg(j)
         transp(0)
         cast_pair(4)
         widen(2)
@@ -358,8 +363,6 @@ def tile_candidateaware_clickednewsattention_pa_t_kernel(
             more = c + 1 < PAIRS
             if c <= LAST_EXIT_ROUND:
                 quant(c + D_QUANT)
-                if c < 2:
-                    gate(c + D_QUANT)
                 new_xg(c + D_EXIT)
                 gmul(c + D_EXIT)
             else:

@@ -15,19 +15,19 @@ AX = mybir.AxisListType
 
 B, N, K, D = 32, 128, 1024, 1024
 P = 128
+BANK = 512
 FLOPS = 2 * B * N * K * D
 
-TUNE = False
 PAIRS = B // 2
-CHUNKS = (2, 2, 4, 2, 6, 16)
-N_WIDE = 4
-D_EXIT = 4
-D_TNEW = 5
-D_QUANT = 2
+X_LOADS = (2, 2, 4, 2, 6, 16)
+ROW_PAIRS = 4
+AHEAD_CAST = 6
+AHEAD_TRANSPOSE = 5
+AHEAD_SCALE = 4
+AHEAD_QUANT = 2
+LAST_SCALE_ROUND = PAIRS - AHEAD_SCALE - 1
 G_MORE = 128
 G_ROWS = G_MORE // 4
-D_CAST = 6
-LAST_EXIT_ROUND = PAIRS - D_EXIT - 1
 ROOT_ROUNDS = (12, 14, 15)
 
 
@@ -60,7 +60,7 @@ def tile_candidateaware_clickednewsattention_pa_t_kernel(
         )
         xbytes = []
         where = []
-        for c, n in enumerate(CHUNKS):
+        for c, n in enumerate(X_LOADS):
             t = const.tile([P, n, K], U8, name="xbytes%d" % c)
             xbytes.append(t)
             for i in range(n):
@@ -72,10 +72,10 @@ def tile_candidateaware_clickednewsattention_pa_t_kernel(
         bias_bc = const.tile([P, D], BF16, name="bias_bc")
 
         def load_x(c):
-            b0 = sum(CHUNKS[:c])
+            b0 = sum(X_LOADS[:c])
             nc.sync.dma_start(
                 out=xbytes[c][:],
-                in_=cand_topics_bytes[b0 : b0 + CHUNKS[c]].rearrange("b n k -> n b k"),
+                in_=cand_topics_bytes[b0 : b0 + X_LOADS[c]].rearrange("b n k -> n b k"),
             )
 
         def load_w(c):
@@ -107,7 +107,6 @@ def tile_candidateaware_clickednewsattention_pa_t_kernel(
         nc.vector.memset(half[:], 0.5)
         warm = const.tile([P, 1], F32, name="warm")
         nc.scalar.activation(out=warm[:], in_=one_col[:], func=ACT.Exp)
-        gate_junk = const.tile([P, 2], U32, name="gate_junk")
         sck = const.tile([P, K + G_MORE], F32, name="sck")
         nc.scalar.copy(
             out=sck[:, 0:K].rearrange("p (g r t) -> p g r t", g=2, t=4),
@@ -130,40 +129,51 @@ def tile_candidateaware_clickednewsattention_pa_t_kernel(
             t = const.tile([P, K], U8, name="wsc%d" % h, align_bytes=64)
             wsc.append(t)
 
-        def transposes(words, base):
+        def transposes(words, base, u_first):
             tp = psum_t.tile([P, 4, P], F32, name="tp")
             for s in range(4):
-                g, u = divmod(s, 2)
+                if u_first:
+                    u, g = divmod(s, 2)
+                else:
+                    g, u = divmod(s, 2)
                 lo = base + 256 * g
                 nc.tensor.transpose(tp[:, s, :], words[:, lo + u : lo + 256 : 2], ident[:])
             return tp
 
-        def wprep(c):
+        def w_transpose(c):
             h, cc = divmod(c, 4)
-            words = wraw[c // 2][:, c % 2, :].bitcast(F32)
-            tp = transposes(words, 0)
+            tp = transposes(wraw[c // 2][:, c % 2, :].bitcast(F32), 0, False)
             dst = wgrp[h][:].bitcast(F32).rearrange("p (g r u) -> p g r u", g=2, u=2)
             nc.scalar.copy(
                 out=dst[:, :, cc * P : (cc + 1) * P, :],
                 in_=tp[:].rearrange("p (g u) r -> p g r u", u=2),
             )
 
-        def quant_w(h):
-            nc.vector.quantize_mx(
-                out=wc[h][:].bitcast(FP8X4), scales=wsc[h][:], in_=wgrp[h][:]
-            )
+        def w_quantize(h):
+            nc.vector.quantize_mx(out=wc[h][:].bitcast(FP8X4), scales=wsc[h][:], in_=wgrp[h][:])
 
         xs_of = {}
+        tp_of = {}
+        xr_of = {}
         xg_of = {}
         xq_of = {}
         acc_of = {}
-        tp_of = {}
+        q_of = {}
 
-        def widen(j):
+        def pair_bytes(j):
+            c, i = where[2 * j]
+            return xbytes[c][:, i : i + 2, :].rearrange("p b k -> p (b k)").bitcast(FP8)
+
+        def new_xg(j):
+            pool = xg_head if j < 2 else xg_pool
+            xg = pool.tile([P, 2 * K], BF16, name="xg", align_bytes=64)
+            xg_of[j] = xg
+
+        def row_product(j):
             xs = xs_pool.tile([P, 2 * K], BF16, name="xs", align_bytes=64)
             xs_of[j] = xs
-            c, i = where[2 * j]
             if j == 0:
+                c, i = where[0]
                 for a in range(2):
                     nc.vector.tensor_tensor(
                         out=xs[:, a * K : (a + 1) * K],
@@ -175,74 +185,27 @@ def tile_candidateaware_clickednewsattention_pa_t_kernel(
                 nc.vector.tensor_tensor(
                     out=xs[:],
                     in0=scale2[:].rearrange("p c k -> p (c k)"),
-                    in1=xbytes[c][:, i : i + 2, :].rearrange("p b k -> p (b k)").bitcast(FP8),
+                    in1=pair_bytes(j),
                     op=ALU.mult,
                 )
 
-        def new_xg(j):
-            if j < 2:
-                xg = xg_head.tile([P, 2 * K], BF16, name="xg", align_bytes=64)
-                xg_of[j] = xg
-            else:
-                xg = xg_pool.tile([P, 2 * K], BF16, name="xg", align_bytes=64)
-                xg_of[j] = xg
-
-        def transp(j):
-            xg = xg_of[j]
+        def row_transpose(j):
             words = xs_of[j][:].bitcast(F32)
-            dst = xg[:].bitcast(F32).rearrange("p (a g r u) -> p a g r u", a=2, g=2, u=2)
-            tps = [transposes(words, 512 * a) for a in range(2)]
+            dst = xg_of[j][:].bitcast(F32).rearrange("p (a g r u) -> p a g r u", a=2, g=2, u=2)
+            tps = [transposes(words, 512 * a, False) for a in range(2)]
             for a in range(2):
-                nc.scalar.copy(
-                    out=dst[:, a], in_=tps[a][:].rearrange("p (g u) r -> p g r u", u=2)
-                )
+                nc.scalar.copy(out=dst[:, a], in_=tps[a][:].rearrange("p (g u) r -> p g r u", u=2))
 
-        whole_cast = {}
-
-        def cast_pair(j):
+        def cast(j):
             xs = xs_pool.tile([P, 2 * K], BF16, name="xs", align_bytes=64)
             xs_of[j] = xs
-            whole_cast[j] = True
-            c, i = where[2 * j]
-            if TUNE:
-                nc.scalar.copy(out=xs[:, 0:K], in_=xbytes[c][:, i, :].bitcast(FP8))
-            else:
-                nc.scalar.copy(
-                    out=xs[:],
-                    in_=xbytes[c][:, i : i + 2, :].rearrange("p b k -> p (b k)").bitcast(FP8),
-                )
+            nc.scalar.copy(out=xs[:], in_=pair_bytes(j))
 
-        def cast_user(j, a):
-            if a == 0:
-                xs = xs_pool.tile([P, 2 * K], BF16, name="xs", align_bytes=64)
-                xs_of[j] = xs
-                whole_cast[j] = False
-            c, i = where[2 * j + a]
-            w = K // 2 if TUNE else K
-            nc.scalar.copy(
-                out=xs_of[j][:, a * K : a * K + w], in_=xbytes[c][:, i, 0:w].bitcast(FP8)
-            )
-
-        def t_new(j):
+        def cast_transpose(j):
             words = xs_of[j][:].bitcast(F32)
-            tps = []
-            for a in range(2):
-                tp = psum_t.tile([P, 4, P], F32, name="tp")
-                for s in range(4):
-                    if a == 0:
-                        g, u = divmod(s, 2)
-                    else:
-                        u, g = divmod(s, 2)
-                    lo = 512 * a + 256 * g
-                    if TUNE:
-                        lo = 256 * g if whole_cast[j] else 512 * a
-                    nc.tensor.transpose(tp[:, s, :], words[:, lo + u : lo + 256 : 2], ident[:])
-                tps.append(tp)
-            tp_of[j] = tps
+            tp_of[j] = [transposes(words, 512 * a, a == 1) for a in range(2)]
 
-        xr_of = {}
-
-        def copy0(j):
+        def copy_unscaled(j):
             xr = xr_pool.tile([P, K + G_MORE], BF16, name="xr", align_bytes=64)
             xr_of[j] = xr
             nc.scalar.copy(
@@ -254,10 +217,14 @@ def tile_candidateaware_clickednewsattention_pa_t_kernel(
                 in_=tp_of[j][1][:, 0:4:2, 0:G_ROWS].rearrange("p u r -> p r u"),
             )
 
-        def exit1(j):
-            xg = xg_of[j]
+        def gpsimd_product(j):
+            nc.gpsimd.tensor_tensor(
+                out=xg_of[j][:, 0 : K + G_MORE], in0=xr_of[j][:], in1=sck[:], op=ALU.mult
+            )
+
+        def vector_product(j):
             nc.vector.tensor_tensor(
-                out=xg[:, K + G_MORE : 2 * K].rearrange("p (m u e) -> p m u e", u=2, e=2),
+                out=xg_of[j][:, K + G_MORE : 2 * K].rearrange("p (m u e) -> p m u e", u=2, e=2),
                 in0=tp_of[j][1][:]
                 .rearrange("p s r -> p (s r)")
                 .bitcast(BF16)
@@ -266,26 +233,16 @@ def tile_candidateaware_clickednewsattention_pa_t_kernel(
                 op=ALU.mult,
             )
 
-        def gmul(j):
-            nc.gpsimd.tensor_tensor(
-                out=xg_of[j][:, 0 : K + G_MORE], in0=xr_of[j][:], in1=sck[:], op=ALU.mult
-            )
-
-        def quant(j):
+        def quantize(j):
             xc = xq_pool.tile([P, 512], U32, name="xc", align_bytes=64)
             xsc = xq_pool.tile([P, 512], U8, name="xsc", align_bytes=64)
             xq_of[j] = (xc, xsc)
             nc.vector.quantize_mx(out=xc[:].bitcast(FP8X4), scales=xsc[:], in_=xg_of[j][:])
 
-        def gate(j):
-            nc.gpsimd.tensor_copy(out=gate_junk[:], in_=xq_of[j][0][:, 0:2])
-
-        q_of = {}
-
-        def mm_group(j, s):
+        def multiply(j, s):
             a, h = divmod(s, 2)
             xc, xsc = xq_of[j]
-            acc = psum_a.tile([P, 512], F32, name="acc")
+            acc = psum_a.tile([P, BANK], F32, name="acc")
             acc_of[(j, s)] = acc
             for g in range(2):
                 c0 = (2 * a + g) * P
@@ -293,37 +250,29 @@ def tile_candidateaware_clickednewsattention_pa_t_kernel(
                     out=acc[:],
                     lhsT=xc[:, c0 : c0 + P].bitcast(FP8X4),
                     lhsT_scale=xsc[:, c0 : c0 + P],
-                    rhs=wc[h][:, g * 512 : (g + 1) * 512].bitcast(FP8X4),
-                    rhs_scale=wsc[h][:, g * 512 : (g + 1) * 512],
+                    rhs=wc[h][:, g * BANK : (g + 1) * BANK].bitcast(FP8X4),
+                    rhs_scale=wsc[h][:, g * BANK : (g + 1) * BANK],
                     start=(g == 0),
                     stop=(g == 1),
                 )
 
-        def q_tile(j, a):
-            if (j, a) not in q_of:
-                if a == 0:
-                    qa = q_pool.tile([P, D], F32, name="qa")
-                    q_of[(j, a)] = qa
-                else:
-                    qb = q_pool.tile([P, D], F32, name="qb")
-                    q_of[(j, a)] = qb
-            return q_of[(j, a)]
-
-        def bias_out(j, s):
+        def add_bias(j, s):
             a, h = divmod(s, 2)
-            q = q_tile(j, a)
+            if h == 0:
+                q = q_pool.tile([P, D], F32, name=("qa", "qb")[a])
+                q_of[(j, a)] = q
             nc.vector.tensor_tensor(
-                out=q[:, h * 512 : (h + 1) * 512],
+                out=q_of[(j, a)][:, h * BANK : (h + 1) * BANK],
                 in0=acc_of[(j, s)][:],
-                in1=bias_bc[:, h * 512 : (h + 1) * 512],
+                in1=bias_bc[:, h * BANK : (h + 1) * BANK],
                 op=ALU.add,
             )
 
-        def square(j, a):
-            i = 2 * j + a
+        def sum_squares(j, a):
+            b = 2 * j + a
             junk = junk_pool.tile([P, D], BF16, name="junk")
             nc.scalar.activation(
-                out=junk[:], in_=q_tile(j, a)[:], func=ACT.Square, accum_out=r2_all[:, i : i + 1]
+                out=junk[:], in_=q_of[(j, a)][:], func=ACT.Square, accum_out=r2_all[:, b : b + 1]
             )
 
         def roots(lo, hi):
@@ -332,99 +281,98 @@ def tile_candidateaware_clickednewsattention_pa_t_kernel(
             )
 
         def store(j, a):
-            nc.sync.dma_start(out=out_0[2 * j + a], in_=q_tile(j, a)[:])
+            nc.sync.dma_start(out=out_0[2 * j + a], in_=q_of[(j, a)][:])
 
-        widen(0)
+        row_product(0)
         for c in range(4):
-            wprep(c)
-        widen(1)
-        for j in range(N_WIDE):
+            w_transpose(c)
+        row_product(1)
+        for j in range(ROW_PAIRS):
             new_xg(j)
-        transp(0)
-        cast_pair(4)
-        widen(2)
-        quant_w(0)
+        row_transpose(0)
+        cast(ROW_PAIRS)
+        row_product(2)
+        w_quantize(0)
         for c in range(4, 8):
-            wprep(c)
-        quant(0)
-        transp(1)
-        widen(3)
-        quant_w(1)
-        quant(1)
-        transp(2)
-        t_new(4)
-        copy0(4)
-        cast_pair(5)
+            w_transpose(c)
+        quantize(0)
+        row_transpose(1)
+        row_product(3)
+        w_quantize(1)
+        quantize(1)
+        row_transpose(2)
+        cast_transpose(ROW_PAIRS)
+        copy_unscaled(ROW_PAIRS)
+        cast(ROW_PAIRS + 1)
         for s in range(4):
-            mm_group(0, s)
+            multiply(0, s)
 
         rooted = 0
         for c in range(PAIRS):
-            more = c + 1 < PAIRS
-            if c <= LAST_EXIT_ROUND:
-                quant(c + D_QUANT)
-                new_xg(c + D_EXIT)
-                gmul(c + D_EXIT)
-            else:
-                first = LAST_EXIT_ROUND + 1 + D_QUANT + 2 * (c - LAST_EXIT_ROUND - 1)
-                for j in range(first, min(first + 2, PAIRS)):
-                    quant(j)
+            if c <= LAST_SCALE_ROUND:
+                quantize(c + AHEAD_QUANT)
+                new_xg(c + AHEAD_SCALE)
+                gpsimd_product(c + AHEAD_SCALE)
+            elif c == LAST_SCALE_ROUND + 1:
+                for j in range(c + AHEAD_QUANT, PAIRS):
+                    quantize(j)
             if c > 0:
-                square(c - 1, 1)
+                sum_squares(c - 1, 1)
             if c in ROOT_ROUNDS:
                 roots(rooted, 2 * c)
                 rooted = 2 * c
-            if c + D_CAST < PAIRS:
-                cast_pair(c + D_CAST)
+            if c + AHEAD_CAST < PAIRS:
+                cast(c + AHEAD_CAST)
             if c == 0:
-                transp(N_WIDE - 1)
-            if c + D_TNEW < PAIRS:
-                t_new(c + D_TNEW)
-                copy0(c + D_TNEW)
+                row_transpose(ROW_PAIRS - 1)
+            if c + AHEAD_TRANSPOSE < PAIRS:
+                cast_transpose(c + AHEAD_TRANSPOSE)
+                copy_unscaled(c + AHEAD_TRANSPOSE)
             for s in range(4):
-                bias_out(c, s)
-                if more:
-                    mm_group(c + 1, s)
-                if s == 0 and c <= LAST_EXIT_ROUND:
-                    exit1(c + D_EXIT)
+                add_bias(c, s)
+                if c + 1 < PAIRS:
+                    multiply(c + 1, s)
+                if s == 0 and c <= LAST_SCALE_ROUND:
+                    vector_product(c + AHEAD_SCALE)
                 if s % 2 == 1:
                     store(c, s // 2)
-            square(c, 0)
+            sum_squares(c, 0)
         roots(rooted, B - 1)
-        q_last = q_tile(PAIRS - 1, 1)
+
+        q_last = q_of[(PAIRS - 1, 1)]
         junk = junk_pool.tile([P, D], BF16, name="junk")
-        part = const.tile([P, 2], F32, name="part")
+        part_s = const.tile([P, 1], F32, name="part_s")
         nc.scalar.activation(
-            out=junk[:, 0:512], in_=q_last[:, 0:512], func=ACT.Square, accum_out=part[:, 0:1]
+            out=junk[:, 0:BANK], in_=q_last[:, 0:BANK], func=ACT.Square, accum_out=part_s[:]
         )
-        junk_v = const.tile([P, 512], BF16, name="junk_v")
+        junk_v = const.tile([P, BANK], BF16, name="junk_v")
         part_v = const.tile([P, 1], F32, name="part_v")
         nc.vector.scalar_tensor_tensor(
             out=junk_v[:],
-            in0=q_last[:, 512:D],
+            in0=q_last[:, BANK:D],
             scalar=1.0,
-            in1=q_last[:, 512:D],
+            in1=q_last[:, BANK:D],
             op0=ALU.mult,
             op1=ALU.mult,
             accum_out=part_v[:],
         )
-        nc.vector.tensor_tensor(
-            out=r2_all[:, B - 1 : B], in0=part[:, 0:1], in1=part_v[:], op=ALU.add
-        )
+        nc.vector.tensor_tensor(out=r2_all[:, B - 1 : B], in0=part_s[:], in1=part_v[:], op=ALU.add)
         roots(B - 1, B)
 
         rt = psum_t.tile([P, 4, P], F32, name="tp")
-        rT = rt[:, 0, :]
-        nc.tensor.transpose(rT, r_all[:], ident[:])
-        nmx = const.tile([P, 1], F32, name="nmx")
-        nc.vector.reduce_max(out=nmx[:], in_=rT, axis=AX.X, negate=True)
+        r_rows = rt[:, 0, :]
+        nc.tensor.transpose(r_rows, r_all[:], ident[:])
+        neg_max = const.tile([P, 1], F32, name="neg_max")
+        nc.vector.reduce_max(out=neg_max[:], in_=r_rows, axis=AX.X, negate=True)
         ex = const.tile([P, P], F32, name="ex")
-        sm = const.tile([P, 1], F32, name="sm")
+        ex_sum = const.tile([P, 1], F32, name="ex_sum")
         nc.scalar.activation(
-            out=ex[:], in_=rT, func=ACT.Exp, bias=nmx[:], scale=1.0, accum_out=sm[:]
+            out=ex[:], in_=r_rows, func=ACT.Exp, bias=neg_max[:], scale=1.0, accum_out=ex_sum[:]
         )
-        rs = const.tile([P, 1], F32, name="rs")
-        nc.vector.reciprocal(out=rs[:], in_=sm[:])
-        wts = const.tile([P, P], F32, name="wts")
-        nc.vector.tensor_scalar(out=wts[:], in0=ex[:], scalar1=rs[:], scalar2=None, op0=ALU.mult)
-        nc.sync.dma_start(out=out_1[:, :], in_=wts[0:B, :])
+        inv_sum = const.tile([P, 1], F32, name="inv_sum")
+        nc.vector.reciprocal(out=inv_sum[:], in_=ex_sum[:])
+        weights = const.tile([P, P], F32, name="weights")
+        nc.vector.tensor_scalar(
+            out=weights[:], in0=ex[:], scalar1=inv_sum[:], scalar2=None, op0=ALU.mult
+        )
+        nc.sync.dma_start(out=out_1[:, :], in_=weights[0:B, :])

@@ -28,7 +28,11 @@ AHEAD_QUANT = 2
 LAST_SCALE_ROUND = PAIRS - AHEAD_SCALE - 1
 G_MORE = 128
 G_ROWS = G_MORE // 4
-ROOT_ROUNDS = (12, 14, 15)
+ROOT_ROUNDS = (12, 14)
+LATE = PAIRS - 1
+PREP = tuple(range(PAIRS - 4)) + (LATE,) + tuple(range(PAIRS - 4, LATE))
+LATE_ROUND = PAIRS - 5
+CHUNKS = D // P
 
 
 def tile_candidateaware_clickednewsattention_pa_t_kernel(
@@ -53,6 +57,9 @@ def tile_candidateaware_clickednewsattention_pa_t_kernel(
             out=sc8[:].rearrange("p (g t) -> p g t", t=4),
             in_=cand_topics_scale.rearrange("a b (g p t) -> p (a b g) t", g=2, p=P, t=4),
         )
+        bias_rows = const.tile([P, P], BF16, name="bias_rows")
+        nc.vector.memset(bias_rows[:], 0.0)
+        nc.scalar.dma_start(out=bias_rows[0:CHUNKS, :], in_=bq.rearrange("(c j) -> c j", j=P))
         scale2 = const.tile([P, 2, K], F32, name="scale2")
         nc.sync.dma_start(
             out=scale2[:, 0, :],
@@ -98,6 +105,8 @@ def tile_candidateaware_clickednewsattention_pa_t_kernel(
 
         ident = const.tile([P, P], F32, name="ident")
         masks.make_identity(nc, ident[:])
+        ident_bf = const.tile([P, P], BF16, name="ident_bf")
+        masks.make_identity(nc, ident_bf[:])
         one_col = const.tile([P, 1], F32, name="one_col")
         nc.vector.memset(one_col[:], 1.0)
         r2_all = const.tile([P, B], F32, name="r2_all")
@@ -283,9 +292,70 @@ def tile_candidateaware_clickednewsattention_pa_t_kernel(
         def store(j, a):
             nc.sync.dma_start(out=out_0[2 * j + a], in_=q_of[(j, a)][:])
 
+        sq_late = const.tile([P, CHUNKS, 2 * P], F32, name="sq_late")
+        late_bank = {}
+
+        def late_multiply(i):
+            xc, xsc = xq_of[LATE]
+            tp = psum_t.tile([P, 4, P], F32, name="tp")
+            late_bank[i] = tp
+            for e in range(2):
+                h, cc = divmod(2 * i + e, 4)
+                for a in range(2):
+                    for g in range(2):
+                        w0 = g * BANK + cc * P
+                        c0 = (2 * a + g) * P
+                        nc.tensor.matmul_mx(
+                            out=tp[:, 2 * e + a, :],
+                            lhsT=wc[h][:, w0 : w0 + P].bitcast(FP8X4),
+                            lhsT_scale=wsc[h][:, w0 : w0 + P],
+                            rhs=xc[:, c0 : c0 + P].bitcast(FP8X4),
+                            rhs_scale=xsc[:, c0 : c0 + P],
+                            start=(g == 0),
+                            stop=(g == 1),
+                        )
+
+        def late_square(i):
+            for e in range(2):
+                c = 2 * i + e
+                nc.scalar.activation(
+                    out=sq_late[:, c, :],
+                    in_=late_bank[i][:, 2 * e : 2 * e + 2, :].rearrange("p a r -> p (a r)"),
+                    func=ACT.Square,
+                    bias=bias_col[:, c : c + 1],
+                    scale=1.0,
+                )
+
+        def late_sum_blocks():
+            tp = psum_t.tile([P, 4, P], F32, name="tp")
+            late_bank["sum"] = tp
+            for a in range(2):
+                for c in range(CHUNKS):
+                    nc.tensor.matmul(
+                        out=tp[:, a, :],
+                        lhsT=sq_late[:, c, a * P : (a + 1) * P],
+                        rhs=ident[:],
+                        is_transpose=True,
+                        start=(c == 0),
+                        stop=(c == CHUNKS - 1),
+                    )
+
+        def late_sum_columns():
+            for a in range(2):
+                b = 2 * LATE + a
+                junk = junk_pool.tile([P, D], BF16, name="junk")
+                nc.scalar.activation(
+                    out=junk[:, 0:P], in_=late_bank["sum"][:, a, :], func=ACT.Copy, accum_out=r2_all[:, b : b + 1]
+                )
+
         row_product(0)
         for c in range(4):
             w_transpose(c)
+        bias_bank = psum_t.tile([P, 4, P], F32, name="tp")
+        bias_turned = bias_bank[:].rearrange("p s r -> p (s r)").bitcast(BF16)[:, 0:P]
+        nc.tensor.transpose(bias_turned, bias_rows[:], ident_bf[:])
+        bias_col = const.tile([P, CHUNKS], F32, name="bias_col")
+        nc.scalar.copy(out=bias_col[:], in_=bias_turned[:, 0:CHUNKS])
         row_product(1)
         for j in range(ROW_PAIRS):
             new_xg(j)
@@ -310,54 +380,71 @@ def tile_candidateaware_clickednewsattention_pa_t_kernel(
         rooted = 0
         for c in range(PAIRS):
             if c <= LAST_SCALE_ROUND:
-                quantize(c + AHEAD_QUANT)
-                new_xg(c + AHEAD_SCALE)
-                gpsimd_product(c + AHEAD_SCALE)
+                quantize(PREP[c + AHEAD_QUANT])
+                new_xg(PREP[c + AHEAD_SCALE])
+                gpsimd_product(PREP[c + AHEAD_SCALE])
             elif c == LAST_SCALE_ROUND + 1:
-                for j in range(c + AHEAD_QUANT, PAIRS):
-                    quantize(j)
-            if c > 0:
+                for i in range(c + AHEAD_QUANT, PAIRS):
+                    quantize(PREP[i])
+            if 0 < c < LATE:
                 sum_squares(c - 1, 1)
             if c in ROOT_ROUNDS:
                 roots(rooted, 2 * c)
                 rooted = 2 * c
+            if c == LATE - 1:
+                roots(2 * LATE, B)
             if c + AHEAD_CAST < PAIRS:
-                cast(c + AHEAD_CAST)
+                cast(PREP[c + AHEAD_CAST])
             if c == 0:
                 row_transpose(ROW_PAIRS - 1)
             if c + AHEAD_TRANSPOSE < PAIRS:
-                cast_transpose(c + AHEAD_TRANSPOSE)
-                copy_unscaled(c + AHEAD_TRANSPOSE)
+                cast_transpose(PREP[c + AHEAD_TRANSPOSE])
+                copy_unscaled(PREP[c + AHEAD_TRANSPOSE])
+            if c == LATE_ROUND:
+                for i in range(3):
+                    late_multiply(i)
+                    late_square(i)
+            if c == LATE_ROUND + 1:
+                late_sum_blocks()
             for s in range(4):
                 add_bias(c, s)
                 if c + 1 < PAIRS:
                     multiply(c + 1, s)
                 if s == 0 and c <= LAST_SCALE_ROUND:
-                    vector_product(c + AHEAD_SCALE)
+                    vector_product(PREP[c + AHEAD_SCALE])
+                if s == 0 and c == LATE_ROUND:
+                    late_multiply(3)
                 if s % 2 == 1:
                     store(c, s // 2)
-            sum_squares(c, 0)
-        roots(rooted, B - 1)
-
-        q_last = q_of[(PAIRS - 1, 1)]
-        junk = junk_pool.tile([P, D], BF16, name="junk")
-        part_s = const.tile([P, 1], F32, name="part_s")
-        nc.scalar.activation(
-            out=junk[:, 0:BANK], in_=q_last[:, 0:BANK], func=ACT.Square, accum_out=part_s[:]
-        )
-        junk_v = const.tile([P, BANK], BF16, name="junk_v")
-        part_v = const.tile([P, 1], F32, name="part_v")
-        nc.vector.scalar_tensor_tensor(
-            out=junk_v[:],
-            in0=q_last[:, BANK:D],
-            scalar=1.0,
-            in1=q_last[:, BANK:D],
-            op0=ALU.mult,
-            op1=ALU.mult,
-            accum_out=part_v[:],
-        )
-        nc.vector.tensor_tensor(out=r2_all[:, B - 1 : B], in0=part_s[:], in1=part_v[:], op=ALU.add)
-        roots(B - 1, B)
+            if c < LATE:
+                sum_squares(c, 0)
+            if c == LATE_ROUND:
+                late_square(3)
+            if c == LATE_ROUND + 1:
+                late_sum_columns()
+            if c == LATE - 1:
+                roots(rooted, 2 * LATE - 1)
+                q_last = q_of[(LATE - 1, 1)]
+                junk = junk_pool.tile([P, D], BF16, name="junk")
+                part_s = const.tile([P, 1], F32, name="part_s")
+                nc.scalar.activation(
+                    out=junk[:, 0:BANK], in_=q_last[:, 0:BANK], func=ACT.Square, accum_out=part_s[:]
+                )
+                junk_v = const.tile([P, BANK], BF16, name="junk_v")
+                part_v = const.tile([P, 1], F32, name="part_v")
+                nc.vector.scalar_tensor_tensor(
+                    out=junk_v[:],
+                    in0=q_last[:, BANK:D],
+                    scalar=1.0,
+                    in1=q_last[:, BANK:D],
+                    op0=ALU.mult,
+                    op1=ALU.mult,
+                    accum_out=part_v[:],
+                )
+                nc.vector.tensor_tensor(
+                    out=r2_all[:, 2 * LATE - 1 : 2 * LATE], in0=part_s[:], in1=part_v[:], op=ALU.add
+                )
+                roots(2 * LATE - 1, 2 * LATE)
 
         rt = psum_t.tile([P, 4, P], F32, name="tp")
         r_rows = rt[:, 0, :]

@@ -28,7 +28,7 @@ AHEAD_QUANT = 2
 LAST_SCALE_ROUND = PAIRS - AHEAD_SCALE - 1
 G_MORE = 128
 G_ROWS = G_MORE // 4
-ROOT_ROUNDS = (12, 14)
+ROOT_ROUNDS = (12, 14, 15)
 LATE = PAIRS - 1
 PREP = tuple(range(PAIRS - 4)) + (LATE,) + tuple(range(PAIRS - 4, LATE))
 LATE_ROUND = PAIRS - 5
@@ -292,35 +292,33 @@ def tile_candidateaware_clickednewsattention_pa_t_kernel(
         def store(j, a):
             nc.sync.dma_start(out=out_0[2 * j + a], in_=q_of[(j, a)][:])
 
-        sq_late = const.tile([P, CHUNKS, 2 * P], F32, name="sq_late")
+        sq_late = const.tile([P, CHUNKS, P], F32, name="sq_late")
         late_bank = {}
 
-        def late_multiply(i):
+        def late_multiply(h):
             xc, xsc = xq_of[LATE]
             tp = psum_t.tile([P, 4, P], F32, name="tp")
-            late_bank[i] = tp
-            for e in range(2):
-                h, cc = divmod(2 * i + e, 4)
-                for a in range(2):
-                    for g in range(2):
-                        w0 = g * BANK + cc * P
-                        c0 = (2 * a + g) * P
-                        nc.tensor.matmul_mx(
-                            out=tp[:, 2 * e + a, :],
-                            lhsT=wc[h][:, w0 : w0 + P].bitcast(FP8X4),
-                            lhsT_scale=wsc[h][:, w0 : w0 + P],
-                            rhs=xc[:, c0 : c0 + P].bitcast(FP8X4),
-                            rhs_scale=xsc[:, c0 : c0 + P],
-                            start=(g == 0),
-                            stop=(g == 1),
-                        )
+            late_bank[h] = tp
+            for cc in range(4):
+                for g in range(2):
+                    w0 = g * BANK + cc * P
+                    c0 = (2 + g) * P
+                    nc.tensor.matmul_mx(
+                        out=tp[:, cc, :],
+                        lhsT=wc[h][:, w0 : w0 + P].bitcast(FP8X4),
+                        lhsT_scale=wsc[h][:, w0 : w0 + P],
+                        rhs=xc[:, c0 : c0 + P].bitcast(FP8X4),
+                        rhs_scale=xsc[:, c0 : c0 + P],
+                        start=(g == 0),
+                        stop=(g == 1),
+                    )
 
-        def late_square(i):
-            for e in range(2):
-                c = 2 * i + e
+        def late_square(h):
+            for cc in range(4):
+                c = 4 * h + cc
                 nc.scalar.activation(
                     out=sq_late[:, c, :],
-                    in_=late_bank[i][:, 2 * e : 2 * e + 2, :].rearrange("p a r -> p (a r)"),
+                    in_=late_bank[h][:, cc, :],
                     func=ACT.Square,
                     bias=bias_col[:, c : c + 1],
                     scale=1.0,
@@ -329,24 +327,21 @@ def tile_candidateaware_clickednewsattention_pa_t_kernel(
         def late_sum_blocks():
             tp = psum_t.tile([P, 4, P], F32, name="tp")
             late_bank["sum"] = tp
-            for a in range(2):
-                for c in range(CHUNKS):
-                    nc.tensor.matmul(
-                        out=tp[:, a, :],
-                        lhsT=sq_late[:, c, a * P : (a + 1) * P],
-                        rhs=ident[:],
-                        is_transpose=True,
-                        start=(c == 0),
-                        stop=(c == CHUNKS - 1),
-                    )
+            for c in range(CHUNKS):
+                nc.tensor.matmul(
+                    out=tp[:, 0, :],
+                    lhsT=sq_late[:, c, :],
+                    rhs=ident[:],
+                    is_transpose=True,
+                    start=(c == 0),
+                    stop=(c == CHUNKS - 1),
+                )
 
         def late_sum_columns():
-            for a in range(2):
-                b = 2 * LATE + a
-                junk = junk_pool.tile([P, D], BF16, name="junk")
-                nc.scalar.activation(
-                    out=junk[:, 0:P], in_=late_bank["sum"][:, a, :], func=ACT.Copy, accum_out=r2_all[:, b : b + 1]
-                )
+            junk = junk_pool.tile([P, D], BF16, name="junk")
+            nc.scalar.activation(
+                out=junk[:, 0:P], in_=late_bank["sum"][:, 0, :], func=ACT.Copy, accum_out=r2_all[:, B - 1 : B]
+            )
 
         row_product(0)
         for c in range(4):
@@ -386,13 +381,13 @@ def tile_candidateaware_clickednewsattention_pa_t_kernel(
             elif c == LAST_SCALE_ROUND + 1:
                 for i in range(c + AHEAD_QUANT, PAIRS):
                     quantize(PREP[i])
-            if 0 < c < LATE:
+            if c > 0:
                 sum_squares(c - 1, 1)
             if c in ROOT_ROUNDS:
                 roots(rooted, 2 * c)
                 rooted = 2 * c
             if c == LATE - 1:
-                roots(2 * LATE, B)
+                roots(B - 1, B)
             if c + AHEAD_CAST < PAIRS:
                 cast(PREP[c + AHEAD_CAST])
             if c == 0:
@@ -401,50 +396,45 @@ def tile_candidateaware_clickednewsattention_pa_t_kernel(
                 cast_transpose(PREP[c + AHEAD_TRANSPOSE])
                 copy_unscaled(PREP[c + AHEAD_TRANSPOSE])
             if c == LATE_ROUND:
-                for i in range(3):
-                    late_multiply(i)
-                    late_square(i)
-            if c == LATE_ROUND + 1:
-                late_sum_blocks()
+                for h in range(2):
+                    late_multiply(h)
+                    late_square(h)
             for s in range(4):
                 add_bias(c, s)
                 if c + 1 < PAIRS:
                     multiply(c + 1, s)
                 if s == 0 and c <= LAST_SCALE_ROUND:
                     vector_product(PREP[c + AHEAD_SCALE])
-                if s == 0 and c == LATE_ROUND:
-                    late_multiply(3)
                 if s % 2 == 1:
                     store(c, s // 2)
+                if c == LATE and s == 1:
+                    q_last = q_of[(LATE, 0)]
+                    junk = junk_pool.tile([P, D], BF16, name="junk")
+                    part_s = const.tile([P, 1], F32, name="part_s")
+                    nc.scalar.activation(
+                        out=junk[:, 0:BANK], in_=q_last[:, 0:BANK], func=ACT.Square, accum_out=part_s[:]
+                    )
+                    junk_v = const.tile([P, BANK], BF16, name="junk_v")
+                    part_v = const.tile([P, 1], F32, name="part_v")
+                    nc.vector.scalar_tensor_tensor(
+                        out=junk_v[:],
+                        in0=q_last[:, BANK:D],
+                        scalar=1.0,
+                        in1=q_last[:, BANK:D],
+                        op0=ALU.mult,
+                        op1=ALU.mult,
+                        accum_out=part_v[:],
+                    )
+                    nc.vector.tensor_tensor(
+                        out=r2_all[:, B - 2 : B - 1], in0=part_s[:], in1=part_v[:], op=ALU.add
+                    )
+                    roots(B - 2, B - 1)
             if c < LATE:
                 sum_squares(c, 0)
             if c == LATE_ROUND:
-                late_square(3)
+                late_sum_blocks()
             if c == LATE_ROUND + 1:
                 late_sum_columns()
-            if c == LATE - 1:
-                roots(rooted, 2 * LATE - 1)
-                q_last = q_of[(LATE - 1, 1)]
-                junk = junk_pool.tile([P, D], BF16, name="junk")
-                part_s = const.tile([P, 1], F32, name="part_s")
-                nc.scalar.activation(
-                    out=junk[:, 0:BANK], in_=q_last[:, 0:BANK], func=ACT.Square, accum_out=part_s[:]
-                )
-                junk_v = const.tile([P, BANK], BF16, name="junk_v")
-                part_v = const.tile([P, 1], F32, name="part_v")
-                nc.vector.scalar_tensor_tensor(
-                    out=junk_v[:],
-                    in0=q_last[:, BANK:D],
-                    scalar=1.0,
-                    in1=q_last[:, BANK:D],
-                    op0=ALU.mult,
-                    op1=ALU.mult,
-                    accum_out=part_v[:],
-                )
-                nc.vector.tensor_tensor(
-                    out=r2_all[:, 2 * LATE - 1 : 2 * LATE], in0=part_s[:], in1=part_v[:], op=ALU.add
-                )
-                roots(2 * LATE - 1, 2 * LATE)
 
         rt = psum_t.tile([P, 4, P], F32, name="tp")
         r_rows = rt[:, 0, :]

@@ -57,9 +57,6 @@ def tile_candidateaware_clickednewsattention_pa_t_kernel(
             out=sc8[:].rearrange("p (g t) -> p g t", t=4),
             in_=cand_topics_scale.rearrange("a b (g p t) -> p (a b g) t", g=2, p=P, t=4),
         )
-        bias_rows = const.tile([P, P], BF16, name="bias_rows")
-        nc.vector.memset(bias_rows[:], 0.0)
-        nc.scalar.dma_start(out=bias_rows[0:CHUNKS, :], in_=bq.rearrange("(c j) -> c j", j=P))
         scale2 = const.tile([P, 2, K], F32, name="scale2")
         nc.sync.dma_start(
             out=scale2[:, 0, :],
@@ -293,6 +290,14 @@ def tile_candidateaware_clickednewsattention_pa_t_kernel(
             nc.sync.dma_start(out=out_0[2 * j + a], in_=q_of[(j, a)][:])
 
         sq_late = const.tile([P, CHUNKS, P], F32, name="sq_late")
+        bias_col = const.tile([P, CHUNKS], F32, name="bias_col")
+
+        def turn_bias():
+            tp = psum_t.tile([P, 4, P], F32, name="tp")
+            turned = tp[:].rearrange("p s r -> p (s r)").bitcast(BF16)
+            for c in range(CHUNKS):
+                nc.tensor.transpose(turned[:, c * P : (c + 1) * P], bias_bc[:, c * P : (c + 1) * P], ident_bf[:])
+            nc.scalar.copy(out=bias_col[:], in_=turned.rearrange("p (c r) -> p c r", r=P)[:, :, 0])
         late_bank = {}
 
         def late_multiply(h):
@@ -346,11 +351,6 @@ def tile_candidateaware_clickednewsattention_pa_t_kernel(
         row_product(0)
         for c in range(4):
             w_transpose(c)
-        bias_bank = psum_t.tile([P, 4, P], F32, name="tp")
-        bias_turned = bias_bank[:].rearrange("p s r -> p (s r)").bitcast(BF16)[:, 0:P]
-        nc.tensor.transpose(bias_turned, bias_rows[:], ident_bf[:])
-        bias_col = const.tile([P, CHUNKS], F32, name="bias_col")
-        nc.scalar.copy(out=bias_col[:], in_=bias_turned[:, 0:CHUNKS])
         row_product(1)
         for j in range(ROW_PAIRS):
             new_xg(j)
@@ -395,6 +395,8 @@ def tile_candidateaware_clickednewsattention_pa_t_kernel(
             if c + AHEAD_TRANSPOSE < PAIRS:
                 cast_transpose(PREP[c + AHEAD_TRANSPOSE])
                 copy_unscaled(PREP[c + AHEAD_TRANSPOSE])
+            if c == LATE_ROUND - 1:
+                turn_bias()
             if c == LATE_ROUND:
                 for h in range(2):
                     late_multiply(h)

@@ -28,9 +28,9 @@ AHEAD_QUANT = 2
 LAST_SCALE_ROUND = PAIRS - AHEAD_SCALE - 1
 G_MORE = 128
 G_ROWS = G_MORE // 4
-ROOT_ROUNDS = (12, 14, 15)
+ROOT_ROUNDS = (12, 14)
 LATE = PAIRS - 1
-PREP = tuple(range(PAIRS - 4)) + (LATE,) + tuple(range(PAIRS - 4, LATE))
+PREP = tuple(range(PAIRS - 5)) + (LATE,) + tuple(range(PAIRS - 5, LATE))
 LATE_ROUND = PAIRS - 5
 CHUNKS = D // P
 
@@ -289,7 +289,8 @@ def tile_candidateaware_clickednewsattention_pa_t_kernel(
         def store(j, a):
             nc.sync.dma_start(out=out_0[2 * j + a], in_=q_of[(j, a)][:])
 
-        sq_late = const.tile([P, CHUNKS, P], F32, name="sq_late")
+        sq_late = const.tile([P, CHUNKS, 2 * P], F32, name="sq_late")
+        late_bank = {}
         bias_col = const.tile([P, CHUNKS], F32, name="bias_col")
 
         def turn_bias():
@@ -298,55 +299,62 @@ def tile_candidateaware_clickednewsattention_pa_t_kernel(
             for c in range(CHUNKS):
                 nc.tensor.transpose(turned[:, c * P : (c + 1) * P], bias_bc[:, c * P : (c + 1) * P], ident_bf[:])
             nc.scalar.copy(out=bias_col[:], in_=turned.rearrange("p (c r) -> p c r", r=P)[:, :, 0])
-        late_bank = {}
 
-        def late_multiply(h):
+        def late_multiply(i):
             xc, xsc = xq_of[LATE]
             tp = psum_t.tile([P, 4, P], F32, name="tp")
-            late_bank[h] = tp
-            for cc in range(4):
-                for g in range(2):
-                    w0 = g * BANK + cc * P
-                    c0 = (2 + g) * P
-                    nc.tensor.matmul_mx(
-                        out=tp[:, cc, :],
-                        lhsT=wc[h][:, w0 : w0 + P].bitcast(FP8X4),
-                        lhsT_scale=wsc[h][:, w0 : w0 + P],
-                        rhs=xc[:, c0 : c0 + P].bitcast(FP8X4),
-                        rhs_scale=xsc[:, c0 : c0 + P],
-                        start=(g == 0),
-                        stop=(g == 1),
-                    )
+            late_bank[i] = tp
+            for e in range(2):
+                h, cc = divmod(2 * i + e, 4)
+                for a in range(2):
+                    for g in range(2):
+                        w0 = g * BANK + cc * P
+                        c0 = (2 * a + g) * P
+                        nc.tensor.matmul_mx(
+                            out=tp[:, 2 * e + a, :],
+                            lhsT=wc[h][:, w0 : w0 + P].bitcast(FP8X4),
+                            lhsT_scale=wsc[h][:, w0 : w0 + P],
+                            rhs=xc[:, c0 : c0 + P].bitcast(FP8X4),
+                            rhs_scale=xsc[:, c0 : c0 + P],
+                            start=(g == 0),
+                            stop=(g == 1),
+                        )
 
-        def late_square(h):
-            for cc in range(4):
-                c = 4 * h + cc
+        def late_square(i):
+            for e in range(2):
+                c = 2 * i + e
                 nc.scalar.activation(
                     out=sq_late[:, c, :],
-                    in_=late_bank[h][:, cc, :],
+                    in_=late_bank[i][:, 2 * e : 2 * e + 2, :].rearrange("p a r -> p (a r)"),
                     func=ACT.Square,
                     bias=bias_col[:, c : c + 1],
                     scale=1.0,
                 )
 
-        def late_sum_blocks():
-            tp = psum_t.tile([P, 4, P], F32, name="tp")
-            late_bank["sum"] = tp
-            for c in range(CHUNKS):
-                nc.tensor.matmul(
-                    out=tp[:, 0, :],
-                    lhsT=sq_late[:, c, :],
-                    rhs=ident[:],
-                    is_transpose=True,
-                    start=(c == 0),
-                    stop=(c == CHUNKS - 1),
-                )
+        def late_sum_blocks(i):
+            if i == 0:
+                for a in range(2):
+                    tp = psum_t.tile([P, 4, P], F32, name="tp")
+                    late_bank[("sum", a)] = tp
+            for e in range(2):
+                c = 2 * i + e
+                for a in range(2):
+                    nc.tensor.matmul(
+                        out=late_bank[("sum", a)][:, 0, :],
+                        lhsT=sq_late[:, c, a * P : (a + 1) * P],
+                        rhs=ident[:],
+                        is_transpose=True,
+                        start=(c == 0),
+                        stop=(c == CHUNKS - 1),
+                    )
 
         def late_sum_columns():
-            junk = junk_pool.tile([P, D], BF16, name="junk")
-            nc.scalar.activation(
-                out=junk[:, 0:P], in_=late_bank["sum"][:, 0, :], func=ACT.Copy, accum_out=r2_all[:, B - 1 : B]
-            )
+            for a in range(2):
+                b = 2 * LATE + a
+                junk = junk_pool.tile([P, D], BF16, name="junk")
+                nc.scalar.activation(
+                    out=junk[:, 0:P], in_=late_bank[("sum", a)][:, 0, :], func=ACT.Copy, accum_out=r2_all[:, b : b + 1]
+                )
 
         row_product(0)
         for c in range(4):
@@ -381,13 +389,20 @@ def tile_candidateaware_clickednewsattention_pa_t_kernel(
             elif c == LAST_SCALE_ROUND + 1:
                 for i in range(c + AHEAD_QUANT, PAIRS):
                     quantize(PREP[i])
-            if c > 0:
+            if 0 < c < LATE:
                 sum_squares(c - 1, 1)
+            if c == LATE_ROUND - 1:
+                late_square(0)
+            if c == LATE_ROUND:
+                late_square(1)
+            if c == LATE_ROUND + 1:
+                late_sum_blocks(3)
+                late_sum_columns()
             if c in ROOT_ROUNDS:
                 roots(rooted, 2 * c)
                 rooted = 2 * c
             if c == LATE - 1:
-                roots(B - 1, B)
+                roots(2 * LATE, B)
             if c + AHEAD_CAST < PAIRS:
                 cast(PREP[c + AHEAD_CAST])
             if c == 0:
@@ -395,48 +410,54 @@ def tile_candidateaware_clickednewsattention_pa_t_kernel(
             if c + AHEAD_TRANSPOSE < PAIRS:
                 cast_transpose(PREP[c + AHEAD_TRANSPOSE])
                 copy_unscaled(PREP[c + AHEAD_TRANSPOSE])
-            if c == LATE_ROUND - 1:
+            if c == LATE_ROUND - 3:
                 turn_bias()
             if c == LATE_ROUND:
-                for h in range(2):
-                    late_multiply(h)
-                    late_square(h)
+                late_multiply(2)
+                late_multiply(3)
+                late_square(2)
             for s in range(4):
                 add_bias(c, s)
                 if c + 1 < PAIRS:
                     multiply(c + 1, s)
                 if s == 0 and c <= LAST_SCALE_ROUND:
                     vector_product(PREP[c + AHEAD_SCALE])
+                if s == 0 and c == LATE_ROUND - 2:
+                    late_multiply(0)
+                if s == 0 and c == LATE_ROUND - 1:
+                    late_multiply(1)
+                if s == 0 and c == LATE_ROUND:
+                    for i in range(3):
+                        late_sum_blocks(i)
                 if s % 2 == 1:
                     store(c, s // 2)
-                if c == LATE and s == 1:
-                    q_last = q_of[(LATE, 0)]
-                    junk = junk_pool.tile([P, D], BF16, name="junk")
-                    part_s = const.tile([P, 1], F32, name="part_s")
-                    nc.scalar.activation(
-                        out=junk[:, 0:BANK], in_=q_last[:, 0:BANK], func=ACT.Square, accum_out=part_s[:]
-                    )
-                    junk_v = const.tile([P, BANK], BF16, name="junk_v")
-                    part_v = const.tile([P, 1], F32, name="part_v")
-                    nc.vector.scalar_tensor_tensor(
-                        out=junk_v[:],
-                        in0=q_last[:, BANK:D],
-                        scalar=1.0,
-                        in1=q_last[:, BANK:D],
-                        op0=ALU.mult,
-                        op1=ALU.mult,
-                        accum_out=part_v[:],
-                    )
-                    nc.vector.tensor_tensor(
-                        out=r2_all[:, B - 2 : B - 1], in0=part_s[:], in1=part_v[:], op=ALU.add
-                    )
-                    roots(B - 2, B - 1)
             if c < LATE:
                 sum_squares(c, 0)
             if c == LATE_ROUND:
-                late_sum_blocks()
-            if c == LATE_ROUND + 1:
-                late_sum_columns()
+                late_square(3)
+            if c == LATE - 1:
+                roots(rooted, 2 * LATE - 1)
+                q_last = q_of[(LATE - 1, 1)]
+                junk = junk_pool.tile([P, D], BF16, name="junk")
+                part_s = const.tile([P, 1], F32, name="part_s")
+                nc.scalar.activation(
+                    out=junk[:, 0:BANK], in_=q_last[:, 0:BANK], func=ACT.Square, accum_out=part_s[:]
+                )
+                junk_v = const.tile([P, BANK], BF16, name="junk_v")
+                part_v = const.tile([P, 1], F32, name="part_v")
+                nc.vector.scalar_tensor_tensor(
+                    out=junk_v[:],
+                    in0=q_last[:, BANK:D],
+                    scalar=1.0,
+                    in1=q_last[:, BANK:D],
+                    op0=ALU.mult,
+                    op1=ALU.mult,
+                    accum_out=part_v[:],
+                )
+                nc.vector.tensor_tensor(
+                    out=r2_all[:, 2 * LATE - 1 : 2 * LATE], in0=part_s[:], in1=part_v[:], op=ALU.add
+                )
+                roots(2 * LATE - 1, 2 * LATE)
 
         rt = psum_t.tile([P, 4, P], F32, name="tp")
         r_rows = rt[:, 0, :]

@@ -380,6 +380,34 @@ def tile_candidateaware_clickednewsattention_pa_t_kernel(
         for s in range(4):
             multiply(0, s)
 
+        ex = const.tile([P, P], F32, name="ex")
+        ex_sum = const.tile([P, 1], F32, name="ex_sum")
+
+        def softmax_head():
+            rt = psum_t.tile([P, 4, P], F32, name="tp")
+            r_rows = rt[:, 0, :]
+            nc.tensor.transpose(r_rows, r_all[:], ident[:])
+            neg_max = const.tile([P, 1], F32, name="neg_max")
+            nc.vector.reduce_max(out=neg_max[:], in_=r_rows, axis=AX.X, negate=True)
+            nc.scalar.activation(
+                out=ex[:], in_=r_rows, func=ACT.Exp, bias=neg_max[:], scale=1.0, accum_out=ex_sum[:]
+            )
+
+        def softmax_end():
+            inv_sum = const.tile([P, 1], F32, name="inv_sum")
+            nc.vector.reciprocal(out=inv_sum[:], in_=ex_sum[:])
+            weights = const.tile([P, P], F32, name="weights")
+            nc.vector.tensor_scalar(
+                out=weights[:], in0=ex[:], scalar1=inv_sum[:], scalar2=None, op0=ALU.mult
+            )
+            nc.sync.dma_start(out=out_1[:, :], in_=weights[0:B, :])
+
+        def store_bank(j, s):
+            a, h = divmod(s, 2)
+            nc.sync.dma_start(
+                out=out_0[2 * j + a][:, h * BANK : (h + 1) * BANK], in_=q_of[(j, a)][:, h * BANK : (h + 1) * BANK]
+            )
+
         rooted = 0
         for c in range(PAIRS):
             if c <= LAST_SCALE_ROUND:
@@ -429,8 +457,12 @@ def tile_candidateaware_clickednewsattention_pa_t_kernel(
                 if s == 0 and c == LATE_ROUND:
                     for i in range(3):
                         late_sum_blocks(i)
-                if s % 2 == 1:
+                if c == LATE:
+                    store_bank(c, s)
+                elif s % 2 == 1:
                     store(c, s // 2)
+                if c == LATE and s == 2:
+                    softmax_head()
             if c < LATE:
                 sum_squares(c, 0)
             if c == LATE_ROUND:
@@ -458,21 +490,4 @@ def tile_candidateaware_clickednewsattention_pa_t_kernel(
                     out=r2_all[:, 2 * LATE - 1 : 2 * LATE], in0=part_s[:], in1=part_v[:], op=ALU.add
                 )
                 roots(2 * LATE - 1, 2 * LATE)
-
-        rt = psum_t.tile([P, 4, P], F32, name="tp")
-        r_rows = rt[:, 0, :]
-        nc.tensor.transpose(r_rows, r_all[:], ident[:])
-        neg_max = const.tile([P, 1], F32, name="neg_max")
-        nc.vector.reduce_max(out=neg_max[:], in_=r_rows, axis=AX.X, negate=True)
-        ex = const.tile([P, P], F32, name="ex")
-        ex_sum = const.tile([P, 1], F32, name="ex_sum")
-        nc.scalar.activation(
-            out=ex[:], in_=r_rows, func=ACT.Exp, bias=neg_max[:], scale=1.0, accum_out=ex_sum[:]
-        )
-        inv_sum = const.tile([P, 1], F32, name="inv_sum")
-        nc.vector.reciprocal(out=inv_sum[:], in_=ex_sum[:])
-        weights = const.tile([P, P], F32, name="weights")
-        nc.vector.tensor_scalar(
-            out=weights[:], in0=ex[:], scalar1=inv_sum[:], scalar2=None, op0=ALU.mult
-        )
-        nc.sync.dma_start(out=out_1[:, :], in_=weights[0:B, :])
+        softmax_end()

@@ -231,11 +231,11 @@ def tile_candidateaware_clickednewsattention_pa_t_kernel(
         def vector_product(j):
             nc.vector.tensor_tensor(
                 out=xg_of[j][:, K + G_MORE : 2 * K].rearrange("p (m u e) -> p m u e", u=2, e=2),
-                in0=tp_of[j][1][:]
+                in0=sck[:, G_MORE:K].rearrange("p (m u e) -> p m u e", u=2, e=2),
+                in1=tp_of[j][1][:]
                 .rearrange("p s r -> p (s r)")
                 .bitcast(BF16)
                 .rearrange("p (u m e) -> p m u e", u=2, e=2)[:, G_ROWS : 2 * P],
-                in1=sck[:, G_MORE:K].rearrange("p (m u e) -> p m u e", u=2, e=2),
                 op=ALU.mult,
             )
 
@@ -269,8 +269,8 @@ def tile_candidateaware_clickednewsattention_pa_t_kernel(
                 q_of[(j, a)] = q
             nc.vector.tensor_tensor(
                 out=q_of[(j, a)][:, h * BANK : (h + 1) * BANK],
-                in0=acc_of[(j, s)][:],
-                in1=bias_bc[:, h * BANK : (h + 1) * BANK],
+                in0=bias_bc[:, h * BANK : (h + 1) * BANK],
+                in1=acc_of[(j, s)][:],
                 op=ALU.add,
             )
 

@@ -19,7 +19,7 @@ BANK = 512
 FLOPS = 2 * B * N * K * D
 
 PAIRS = B // 2
-X_LOADS = (2, 2, 4, 2, 6, 16)
+X_LOADS = (4, 4, 2, 6, 16)
 ROW_PAIRS = 4
 AHEAD_CAST = 6
 AHEAD_TRANSPOSE = 5
@@ -89,16 +89,15 @@ def tile_candidateaware_clickednewsattention_pa_t_kernel(
             )
 
         load_x(0)
-        load_x(1)
         load_w(0)
         load_w(1)
+        load_x(1)
         load_x(2)
-        load_x(3)
         load_w(2)
         load_w(3)
-        load_x(4)
+        load_x(3)
         nc.sync.dma_start(out=bias_bc[:], in_=bq.partition_broadcast(P))
-        load_x(5)
+        load_x(4)
 
         ident = const.tile([P, P], F32, name="ident")
         masks.make_identity(nc, ident[:])

@@ -460,7 +460,7 @@ def tile_candidateaware_clickednewsattention_pa_t_kernel(
                     store_bank(c, s)
                 elif s % 2 == 1:
                     store(c, s // 2)
-                if c == LATE and s == 2:
+                if c == LATE and s == 3:
                     softmax_head()
             if c < LATE:
                 sum_squares(c, 0)
@@ -468,25 +468,6 @@ def tile_candidateaware_clickednewsattention_pa_t_kernel(
                 late_square(3)
             if c == LATE - 1:
                 roots(rooted, 2 * LATE - 1)
-                q_last = q_of[(LATE - 1, 1)]
-                junk = junk_pool.tile([P, D], BF16, name="junk")
-                part_s = const.tile([P, 1], F32, name="part_s")
-                nc.scalar.activation(
-                    out=junk[:, 0:BANK], in_=q_last[:, 0:BANK], func=ACT.Square, accum_out=part_s[:]
-                )
-                junk_v = const.tile([P, BANK], BF16, name="junk_v")
-                part_v = const.tile([P, 1], F32, name="part_v")
-                nc.vector.scalar_tensor_tensor(
-                    out=junk_v[:],
-                    in0=q_last[:, BANK:D],
-                    scalar=1.0,
-                    in1=q_last[:, BANK:D],
-                    op0=ALU.mult,
-                    op1=ALU.mult,
-                    accum_out=part_v[:],
-                )
-                nc.vector.tensor_tensor(
-                    out=r2_all[:, 2 * LATE - 1 : 2 * LATE], in0=part_s[:], in1=part_v[:], op=ALU.add
-                )
+                sum_squares(LATE - 1, 1)
                 roots(2 * LATE - 1, 2 * LATE)
         softmax_end()

@@ -21,6 +21,8 @@ FLOPS = 2 * B * N * K * D
 PAIRS = B // 2
 X_LOADS = (4, 4, 2, 6, 16)
 ROW_PAIRS = 4
+HEAD_PAIRS = 2
+HEAD_ROWS = 96
 AHEAD_CAST = 6
 AHEAD_TRANSPOSE = 5
 AHEAD_SCALE = 4
@@ -57,11 +59,7 @@ def tile_candidateaware_clickednewsattention_pa_t_kernel(
             out=sc8[:].rearrange("p (g t) -> p g t", t=4),
             in_=cand_topics_scale.rearrange("a b (g p t) -> p (a b g) t", g=2, p=P, t=4),
         )
-        scale2 = const.tile([P, 2, K], F32, name="scale2")
-        nc.sync.dma_start(
-            out=scale2[:, 0, :],
-            in_=cand_topics_scale.rearrange("a b k -> (a b k)").partition_broadcast(P),
-        )
+        scale_bc = const.tile([P, K], F32, name="scale_bc")
         xbytes = []
         where = []
         for c, n in enumerate(X_LOADS):
@@ -89,6 +87,9 @@ def tile_candidateaware_clickednewsattention_pa_t_kernel(
             )
 
         load_x(0)
+        nc.sync.dma_start(
+            out=scale_bc[:], in_=cand_topics_scale.rearrange("a b k -> (a b k)").partition_broadcast(P)
+        )
         load_w(0)
         load_w(1)
         load_x(1)
@@ -121,7 +122,6 @@ def tile_candidateaware_clickednewsattention_pa_t_kernel(
             out=sck[:, K : K + G_MORE].rearrange("p (r t) -> p r t", t=4),
             in_=sc8[:, 0:4].unsqueeze(1).to_broadcast([P, G_ROWS, 4]),
         )
-        nc.scalar.copy(out=scale2[:, 1, :], in_=scale2[:, 0, :])
 
         wgrp = []
         wc = []
@@ -177,20 +177,12 @@ def tile_candidateaware_clickednewsattention_pa_t_kernel(
         def row_product(j):
             xs = xs_pool.tile([P, 2 * K], BF16, name="xs", align_bytes=64)
             xs_of[j] = xs
-            if j == 0:
-                c, i = where[0]
-                for a in range(2):
-                    nc.vector.tensor_tensor(
-                        out=xs[:, a * K : (a + 1) * K],
-                        in0=scale2[:, 0, :],
-                        in1=xbytes[c][:, i + a, :].bitcast(FP8),
-                        op=ALU.mult,
-                    )
-            else:
+            c, i = where[2 * j]
+            for a in range(2):
                 nc.vector.tensor_tensor(
-                    out=xs[:],
-                    in0=scale2[:].rearrange("p c k -> p (c k)"),
-                    in1=pair_bytes(j),
+                    out=xs[:, a * K : (a + 1) * K],
+                    in0=scale_bc[:],
+                    in1=xbytes[c][:, i + a, :].bitcast(FP8),
                     op=ALU.mult,
                 )
 
@@ -235,6 +227,41 @@ def tile_candidateaware_clickednewsattention_pa_t_kernel(
                 .rearrange("p s r -> p (s r)")
                 .bitcast(BF16)
                 .rearrange("p (u m e) -> p m u e", u=2, e=2)[:, G_ROWS : 2 * P],
+                op=ALU.mult,
+            )
+
+        def head_cast(j, a):
+            if a == 0:
+                xs = xs_pool.tile([P, 2 * K], BF16, name="xs", align_bytes=64)
+                xs_of[j] = xs
+            c, i = where[2 * j + a]
+            nc.scalar.copy(out=xs_of[j][:, a * K : (a + 1) * K], in_=xbytes[c][:, i, :].bitcast(FP8))
+
+        def head_transpose(j):
+            words = xs_of[j][:].bitcast(F32)
+            tp_of[j] = [transposes(words, 512 * a, True) for a in range(2)]
+
+        def head_copy(j):
+            xr = xr_pool.tile([P, K + G_MORE], BF16, name="xr", align_bytes=64)
+            xr_of[j] = xr
+            nc.scalar.copy(
+                out=xr[:, 0 : 4 * HEAD_ROWS].bitcast(F32).rearrange("p (m u) -> p m u", u=2),
+                in_=tp_of[j][0][:].rearrange("p s r -> p (s r)").rearrange("p (u m) -> p m u", u=2)[:, 0:HEAD_ROWS, :],
+            )
+
+        def head_gpsimd(j):
+            n = 4 * HEAD_ROWS
+            nc.gpsimd.tensor_tensor(out=xg_of[j][:, 0:n], in0=xr_of[j][:, 0:n], in1=sck[:, 0:n], op=ALU.mult)
+
+        def head_vector(j, a):
+            m0 = HEAD_ROWS if a == 0 else 0
+            nc.vector.tensor_tensor(
+                out=xg_of[j][:, a * K + 4 * m0 : (a + 1) * K].rearrange("p (m u e) -> p m u e", u=2, e=2),
+                in0=sck[:, 4 * m0 : K].rearrange("p (m u e) -> p m u e", u=2, e=2),
+                in1=tp_of[j][a][:]
+                .rearrange("p s r -> p (s r)")
+                .bitcast(BF16)
+                .rearrange("p (u m e) -> p m u e", u=2, e=2)[:, m0 : 2 * P],
                 op=ALU.mult,
             )
 
@@ -355,20 +382,28 @@ def tile_candidateaware_clickednewsattention_pa_t_kernel(
                     out=junk[:, 0:P], in_=late_bank[("sum", a)][:, 0, :], func=ACT.Copy, accum_out=r2_all[:, b : b + 1]
                 )
 
-        row_product(0)
-        for c in range(4):
-            w_transpose(c)
-        row_product(1)
         for j in range(ROW_PAIRS):
             new_xg(j)
-        row_transpose(0)
+        head_cast(0, 0)
+        head_cast(0, 1)
+        head_transpose(0)
+        head_cast(1, 0)
+        head_cast(1, 1)
+        for j in range(HEAD_PAIRS):
+            if j > 0:
+                head_transpose(j)
+            head_copy(j)
+            head_gpsimd(j)
+            head_vector(j, 0)
+            head_vector(j, 1)
+        for c in range(4):
+            w_transpose(c)
         cast(ROW_PAIRS)
         row_product(2)
         w_quantize(0)
         for c in range(4, 8):
             w_transpose(c)
         quantize(0)
-        row_transpose(1)
         row_product(3)
         w_quantize(1)
         quantize(1)

@@ -231,34 +231,32 @@ def tile_candidateaware_clickednewsattention_pa_t_kernel(
             )
 
         def head_cast(j, a):
-            if a == 0:
-                xs = xs_pool.tile([P, 2 * K], BF16, name="xs", align_bytes=64)
-                xs_of[j] = xs
+            xs = xs_pool.tile([P, K], BF16, name="xs", align_bytes=64)
+            xs_of[(j, a)] = xs
             c, i = where[2 * j + a]
-            nc.scalar.copy(out=xs_of[j][:, a * K : (a + 1) * K], in_=xbytes[c][:, i, :].bitcast(FP8))
+            nc.scalar.copy(out=xs[:], in_=xbytes[c][:, i, :].bitcast(FP8))
 
-        def head_transpose(j):
-            words = xs_of[j][:].bitcast(F32)
-            tp_of[j] = [transposes(words, 512 * a, True) for a in range(2)]
+        def head_transpose(j, a):
+            tp_of[(j, a)] = transposes(xs_of[(j, a)][:].bitcast(F32), 0, True)
 
         def head_copy(j):
             xr = xr_pool.tile([P, K + G_MORE], BF16, name="xr", align_bytes=64)
             xr_of[j] = xr
             nc.scalar.copy(
                 out=xr[:, 0 : 4 * HEAD_ROWS].bitcast(F32).rearrange("p (m u) -> p m u", u=2),
-                in_=tp_of[j][0][:].rearrange("p s r -> p (s r)").rearrange("p (u m) -> p m u", u=2)[:, 0:HEAD_ROWS, :],
+                in_=tp_of[(j, 1)][:].rearrange("p s r -> p (s r)").rearrange("p (u m) -> p m u", u=2)[:, 0:HEAD_ROWS, :],
             )
 
         def head_gpsimd(j):
             n = 4 * HEAD_ROWS
-            nc.gpsimd.tensor_tensor(out=xg_of[j][:, 0:n], in0=xr_of[j][:, 0:n], in1=sck[:, 0:n], op=ALU.mult)
+            nc.gpsimd.tensor_tensor(out=xg_of[j][:, K : K + n], in0=xr_of[j][:, 0:n], in1=sck[:, 0:n], op=ALU.mult)
 
         def head_vector(j, a):
-            m0 = HEAD_ROWS if a == 0 else 0
+            m0 = HEAD_ROWS if a == 1 else 0
             nc.vector.tensor_tensor(
                 out=xg_of[j][:, a * K + 4 * m0 : (a + 1) * K].rearrange("p (m u e) -> p m u e", u=2, e=2),
                 in0=sck[:, 4 * m0 : K].rearrange("p (m u e) -> p m u e", u=2, e=2),
-                in1=tp_of[j][a][:]
+                in1=tp_of[(j, a)][:]
                 .rearrange("p s r -> p (s r)")
                 .bitcast(BF16)
                 .rearrange("p (u m e) -> p m u e", u=2, e=2)[:, m0 : 2 * P],
@@ -385,17 +383,21 @@ def tile_candidateaware_clickednewsattention_pa_t_kernel(
         for j in range(ROW_PAIRS):
             new_xg(j)
         head_cast(0, 0)
+        head_transpose(0, 0)
         head_cast(0, 1)
-        head_transpose(0)
+        head_transpose(0, 1)
         head_cast(1, 0)
+        head_vector(0, 0)
+        head_copy(0)
+        head_gpsimd(0)
+        head_transpose(1, 0)
         head_cast(1, 1)
-        for j in range(HEAD_PAIRS):
-            if j > 0:
-                head_transpose(j)
-            head_copy(j)
-            head_gpsimd(j)
-            head_vector(j, 0)
-            head_vector(j, 1)
+        head_vector(0, 1)
+        head_transpose(1, 1)
+        head_vector(1, 0)
+        head_copy(1)
+        head_gpsimd(1)
+        head_vector(1, 1)
         for c in range(4):
             w_transpose(c)
         cast(ROW_PAIRS)

@@ -20,8 +20,7 @@ FLOPS = 2 * B * N * K * D
 
 PAIRS = B // 2
 X_LOADS = (4, 4, 2, 6, 16)
-ROW_PAIRS = 4
-HEAD_PAIRS = 2
+HEAD_PAIRS = 4
 HEAD_ROWS = 96
 AHEAD_CAST = 6
 AHEAD_TRANSPOSE = 5
@@ -59,7 +58,6 @@ def tile_candidateaware_clickednewsattention_pa_t_kernel(
             out=sc8[:].rearrange("p (g t) -> p g t", t=4),
             in_=cand_topics_scale.rearrange("a b (g p t) -> p (a b g) t", g=2, p=P, t=4),
         )
-        scale_bc = const.tile([P, K], F32, name="scale_bc")
         xbytes = []
         where = []
         for c, n in enumerate(X_LOADS):
@@ -87,15 +85,12 @@ def tile_candidateaware_clickednewsattention_pa_t_kernel(
             )
 
         load_x(0)
-        nc.sync.dma_start(
-            out=scale_bc[:], in_=cand_topics_scale.rearrange("a b k -> (a b k)").partition_broadcast(P)
-        )
         load_w(0)
-        load_w(1)
         load_x(1)
-        load_x(2)
+        load_w(1)
         load_w(2)
         load_w(3)
+        load_x(2)
         load_x(3)
         nc.sync.dma_start(out=bias_bc[:], in_=bq.partition_broadcast(P))
         load_x(4)
@@ -114,11 +109,11 @@ def tile_candidateaware_clickednewsattention_pa_t_kernel(
         warm = const.tile([P, 1], F32, name="warm")
         nc.scalar.activation(out=warm[:], in_=one_col[:], func=ACT.Exp)
         sck = const.tile([P, K + G_MORE], F32, name="sck")
-        nc.scalar.copy(
+        nc.vector.tensor_copy(
             out=sck[:, 0:K].rearrange("p (g r t) -> p g r t", g=2, t=4),
             in_=sc8[:].rearrange("p (g t) -> p g t", t=4).unsqueeze(2).to_broadcast([P, 2, P, 4]),
         )
-        nc.scalar.copy(
+        nc.vector.tensor_copy(
             out=sck[:, K : K + G_MORE].rearrange("p (r t) -> p r t", t=4),
             in_=sc8[:, 0:4].unsqueeze(1).to_broadcast([P, G_ROWS, 4]),
         )
@@ -134,8 +129,11 @@ def tile_candidateaware_clickednewsattention_pa_t_kernel(
             t = const.tile([P, K], U8, name="wsc%d" % h, align_bytes=64)
             wsc.append(t)
 
-        def transposes(words, base, u_first):
-            tp = psum_t.tile([P, 4, P], F32, name="tp")
+        def transposes(words, base, u_first, sums_bank=False):
+            if sums_bank:
+                tp = psum_a.tile([P, 4, P], F32, name="acc")
+            else:
+                tp = psum_t.tile([P, 4, P], F32, name="tp")
             for s in range(4):
                 if u_first:
                     u, g = divmod(s, 2)
@@ -147,7 +145,7 @@ def tile_candidateaware_clickednewsattention_pa_t_kernel(
 
         def w_transpose(c):
             h, cc = divmod(c, 4)
-            tp = transposes(wraw[c // 2][:, c % 2, :].bitcast(F32), 0, False)
+            tp = transposes(wraw[c // 2][:, c % 2, :].bitcast(F32), 0, False, True)
             dst = wgrp[h][:].bitcast(F32).rearrange("p (g r u) -> p g r u", g=2, u=2)
             nc.scalar.copy(
                 out=dst[:, :, cc * P : (cc + 1) * P, :],
@@ -173,25 +171,6 @@ def tile_candidateaware_clickednewsattention_pa_t_kernel(
             pool = xg_head if j < 2 else xg_pool
             xg = pool.tile([P, 2 * K], BF16, name="xg", align_bytes=64)
             xg_of[j] = xg
-
-        def row_product(j):
-            xs = xs_pool.tile([P, 2 * K], BF16, name="xs", align_bytes=64)
-            xs_of[j] = xs
-            c, i = where[2 * j]
-            for a in range(2):
-                nc.vector.tensor_tensor(
-                    out=xs[:, a * K : (a + 1) * K],
-                    in0=scale_bc[:],
-                    in1=xbytes[c][:, i + a, :].bitcast(FP8),
-                    op=ALU.mult,
-                )
-
-        def row_transpose(j):
-            words = xs_of[j][:].bitcast(F32)
-            dst = xg_of[j][:].bitcast(F32).rearrange("p (a g r u) -> p a g r u", a=2, g=2, u=2)
-            tps = [transposes(words, 512 * a, False) for a in range(2)]
-            for a in range(2):
-                nc.scalar.copy(out=dst[:, a], in_=tps[a][:].rearrange("p (g u) r -> p g r u", u=2))
 
         def cast(j):
             xs = xs_pool.tile([P, 2 * K], BF16, name="xs", align_bytes=64)
@@ -380,7 +359,7 @@ def tile_candidateaware_clickednewsattention_pa_t_kernel(
                     out=junk[:, 0:P], in_=late_bank[("sum", a)][:, 0, :], func=ACT.Copy, accum_out=r2_all[:, b : b + 1]
                 )
 
-        for j in range(ROW_PAIRS):
+        for j in range(HEAD_PAIRS):
             new_xg(j)
         head_cast(0, 0)
         head_transpose(0, 0)
@@ -398,21 +377,36 @@ def tile_candidateaware_clickednewsattention_pa_t_kernel(
         head_copy(1)
         head_gpsimd(1)
         head_vector(1, 1)
-        for c in range(4):
-            w_transpose(c)
-        cast(ROW_PAIRS)
-        row_product(2)
-        w_quantize(0)
+        head_cast(2, 0)
+        head_cast(2, 1)
+        w_transpose(0)
+        w_transpose(1)
+        head_transpose(2, 0)
+        head_transpose(2, 1)
+        head_vector(2, 0)
+        head_copy(2)
+        head_gpsimd(2)
+        head_vector(2, 1)
+        head_cast(3, 0)
+        head_cast(3, 1)
+        w_transpose(2)
+        w_transpose(3)
+        head_transpose(3, 0)
+        head_transpose(3, 1)
+        head_vector(3, 0)
+        head_copy(3)
+        head_gpsimd(3)
+        head_vector(3, 1)
+        cast(HEAD_PAIRS)
         for c in range(4, 8):
             w_transpose(c)
+        w_quantize(0)
         quantize(0)
-        row_product(3)
+        cast_transpose(HEAD_PAIRS)
+        copy_unscaled(HEAD_PAIRS)
         w_quantize(1)
         quantize(1)
-        row_transpose(2)
-        cast_transpose(ROW_PAIRS)
-        copy_unscaled(ROW_PAIRS)
-        cast(ROW_PAIRS + 1)
+        cast(HEAD_PAIRS + 1)
         for s in range(4):
             multiply(0, s)
 
@@ -469,8 +463,6 @@ def tile_candidateaware_clickednewsattention_pa_t_kernel(
                 roots(2 * LATE, B)
             if c + AHEAD_CAST < PAIRS:
                 cast(PREP[c + AHEAD_CAST])
-            if c == 0:
-                row_transpose(ROW_PAIRS - 1)
             if c + AHEAD_TRANSPOSE < PAIRS:
                 cast_transpose(PREP[c + AHEAD_TRANSPOSE])
                 copy_unscaled(PREP[c + AHEAD_TRANSPOSE])

@@ -19,7 +19,7 @@ BANK = 512
 FLOPS = 2 * B * N * K * D
 
 PAIRS = B // 2
-X_LOADS = (4, 4, 2, 6, 16)
+X_LOADS = (2, 2, 4, 2, 6, 16)
 HEAD_PAIRS = 4
 HEAD_ROWS = 96
 AHEAD_CAST = 6
@@ -85,15 +85,16 @@ def tile_candidateaware_clickednewsattention_pa_t_kernel(
             )
 
         load_x(0)
-        load_w(0)
         load_x(1)
+        load_w(0)
+        load_x(2)
         load_w(1)
         load_w(2)
         load_w(3)
-        load_x(2)
         load_x(3)
-        nc.sync.dma_start(out=bias_bc[:], in_=bq.partition_broadcast(P))
         load_x(4)
+        nc.sync.dma_start(out=bias_bc[:], in_=bq.partition_broadcast(P))
+        load_x(5)
 
         ident = const.tile([P, P], F32, name="ident")
         masks.make_identity(nc, ident[:])
@@ -404,8 +405,8 @@ def tile_candidateaware_clickednewsattention_pa_t_kernel(
         quantize(0)
         cast_transpose(HEAD_PAIRS)
         copy_unscaled(HEAD_PAIRS)
-        w_quantize(1)
         quantize(1)
+        w_quantize(1)
         cast(HEAD_PAIRS + 1)
         for s in range(4):
             multiply(0, s)

@@ -34,6 +34,7 @@ LATE = PAIRS - 1
 PREP = tuple(range(PAIRS - 5)) + (LATE,) + tuple(range(PAIRS - 5, LATE))
 LATE_ROUND = PAIRS - 5
 CHUNKS = D // P
+WARM_MATMULS = 6
 
 
 def tile_candidateaware_clickednewsattention_pa_t_kernel(
@@ -102,6 +103,11 @@ def tile_candidateaware_clickednewsattention_pa_t_kernel(
         masks.make_identity(nc, ident_bf[:])
         one_col = const.tile([P, 1], F32, name="one_col")
         nc.vector.memset(one_col[:], 1.0)
+        ones_bf = const.tile([P, BANK], BF16, name="ones_bf")
+        nc.vector.memset(ones_bf[:], 1.0)
+        for i in range(WARM_MATMULS):
+            acc = psum_a.tile([P, BANK], F32, name="acc")
+            nc.tensor.matmul(out=acc[:], lhsT=ones_bf[:, 0:P], rhs=ones_bf[:], start=True, stop=True)
         r2_all = const.tile([P, B], F32, name="r2_all")
         r_all = const.tile([P, P], F32, name="r_all")
         nc.vector.memset(r_all[:], 1.0)

@@ -87,8 +87,8 @@ def tile_candidateaware_clickednewsattention_pa_t_kernel(
 
         load_x(0)
         load_x(1)
-        load_w(0)
         load_x(2)
+        load_w(0)
         load_w(1)
         load_w(2)
         load_w(3)
@@ -380,30 +380,30 @@ def tile_candidateaware_clickednewsattention_pa_t_kernel(
         head_cast(1, 1)
         head_vector(0, 1)
         head_transpose(1, 1)
+        head_cast(2, 0)
         head_vector(1, 0)
         head_copy(1)
         head_gpsimd(1)
         head_vector(1, 1)
-        head_cast(2, 0)
         head_cast(2, 1)
         w_transpose(0)
-        w_transpose(1)
         head_transpose(2, 0)
         head_transpose(2, 1)
+        head_cast(3, 0)
         head_vector(2, 0)
         head_copy(2)
         head_gpsimd(2)
         head_vector(2, 1)
-        head_cast(3, 0)
         head_cast(3, 1)
-        w_transpose(2)
-        w_transpose(3)
+        w_transpose(1)
         head_transpose(3, 0)
         head_transpose(3, 1)
+        w_transpose(2)
         head_vector(3, 0)
         head_copy(3)
         head_gpsimd(3)
         head_vector(3, 1)
+        w_transpose(3)
         cast(HEAD_PAIRS)
         for c in range(4, 8):
             w_transpose(c)

@@ -90,9 +90,9 @@ def tile_candidateaware_clickednewsattention_pa_t_kernel(
         load_x(2)
         load_w(0)
         load_w(1)
+        load_x(3)
         load_w(2)
         load_w(3)
-        load_x(3)
         load_x(4)
         nc.sync.dma_start(out=bias_bc[:], in_=bq.partition_broadcast(P))
         load_x(5)
@@ -220,7 +220,10 @@ def tile_candidateaware_clickednewsattention_pa_t_kernel(
             xs = xs_pool.tile([P, K], BF16, name="xs", align_bytes=64)
             xs_of[(j, a)] = xs
             c, i = where[2 * j + a]
-            nc.scalar.copy(out=xs[:], in_=xbytes[c][:, i, :].bitcast(FP8))
+            if (j, a) == (0, 1):
+                nc.vector.tensor_copy(out=xs[:], in_=xbytes[c][:, i, :].bitcast(FP8))
+            else:
+                nc.scalar.copy(out=xs[:], in_=xbytes[c][:, i, :].bitcast(FP8))
 
         def head_transpose(j, a):
             tp_of[(j, a)] = transposes(xs_of[(j, a)][:].bitcast(F32), 0, True)
@@ -373,19 +376,19 @@ def tile_candidateaware_clickednewsattention_pa_t_kernel(
         head_cast(0, 1)
         head_transpose(0, 1)
         head_cast(1, 0)
+        head_transpose(1, 0)
+        head_cast(1, 1)
         head_vector(0, 0)
         head_copy(0)
         head_gpsimd(0)
-        head_transpose(1, 0)
-        head_cast(1, 1)
         head_vector(0, 1)
         head_transpose(1, 1)
         head_cast(2, 0)
+        head_cast(2, 1)
         head_vector(1, 0)
         head_copy(1)
         head_gpsimd(1)
         head_vector(1, 1)
-        head_cast(2, 1)
         w_transpose(0)
         head_transpose(2, 0)
         head_transpose(2, 1)

@@ -401,11 +401,11 @@ def tile_candidateaware_clickednewsattention_pa_t_kernel(
         w_transpose(1)
         head_transpose(3, 0)
         head_transpose(3, 1)
-        w_transpose(2)
         head_vector(3, 0)
         head_copy(3)
         head_gpsimd(3)
         head_vector(3, 1)
+        w_transpose(2)
         w_transpose(3)
         cast(HEAD_PAIRS)
         for c in range(4, 8):

@@ -27,7 +27,7 @@ AHEAD_TRANSPOSE = 5
 AHEAD_SCALE = 4
 AHEAD_QUANT = 2
 LAST_SCALE_ROUND = PAIRS - AHEAD_SCALE - 1
-G_MORE = 128
+G_MORE = 192
 G_ROWS = G_MORE // 4
 ROOT_ROUNDS = (12, 14)
 LATE = PAIRS - 1
@@ -125,6 +125,11 @@ def tile_candidateaware_clickednewsattention_pa_t_kernel(
             in_=sc8[:, 0:4].unsqueeze(1).to_broadcast([P, G_ROWS, 4]),
         )
 
+        sck_g = const.tile([P, K + G_MORE], F32, name="sck_g")
+
+        def build_sck_g():
+            nc.vector.tensor_copy(out=sck_g[:], in_=sck[:])
+
         wgrp = []
         wc = []
         wsc = []
@@ -202,7 +207,7 @@ def tile_candidateaware_clickednewsattention_pa_t_kernel(
 
         def gpsimd_product(j):
             nc.gpsimd.tensor_tensor(
-                out=xg_of[j][:, 0 : K + G_MORE], in0=xr_of[j][:], in1=sck[:], op=ALU.mult
+                out=xg_of[j][:, 0 : K + G_MORE], in0=xr_of[j][:], in1=sck_g[:], op=ALU.mult
             )
 
         def vector_product(j):
@@ -238,7 +243,7 @@ def tile_candidateaware_clickednewsattention_pa_t_kernel(
 
         def head_gpsimd(j):
             n = 4 * HEAD_ROWS
-            nc.gpsimd.tensor_tensor(out=xg_of[j][:, K : K + n], in0=xr_of[j][:, 0:n], in1=sck[:, 0:n], op=ALU.mult)
+            nc.gpsimd.tensor_tensor(out=xg_of[j][:, K : K + n], in0=xr_of[j][:, 0:n], in1=sck_g[:, 0:n], op=ALU.mult)
 
         def head_vector(j, a):
             m0 = HEAD_ROWS if a == 1 else 0
@@ -374,6 +379,7 @@ def tile_candidateaware_clickednewsattention_pa_t_kernel(
         head_cast(0, 0)
         head_transpose(0, 0)
         head_cast(0, 1)
+        build_sck_g()
         head_transpose(0, 1)
         head_cast(1, 0)
         head_transpose(1, 0)

@@ -27,7 +27,7 @@ AHEAD_TRANSPOSE = 5
 AHEAD_SCALE = 4
 AHEAD_QUANT = 2
 LAST_SCALE_ROUND = PAIRS - AHEAD_SCALE - 1
-G_MORE = 192
+G_MORE = 160
 G_ROWS = G_MORE // 4
 ROOT_ROUNDS = (12, 14)
 LATE = PAIRS - 1

from contextlib import ExitStack

import concourse.masks as masks
import concourse.mybir as mybir

F32 = mybir.dt.float32
BF16 = mybir.dt.bfloat16
U32 = mybir.dt.uint32
U8 = mybir.dt.uint8
FP8 = mybir.dt.float8_e4m3fn
FP8X4 = mybir.dt.float8_e4m3fn_x4
ALU = mybir.AluOpType
ACT = mybir.ActivationFunctionType
AX = mybir.AxisListType

B, N, K, D = 32, 128, 1024, 1024
P = 128
BANK = 512
FLOPS = 2 * B * N * K * D

PAIRS = B // 2
X_LOADS = (2, 2, 4, 2, 6, 16)
HEAD_PAIRS = 4
HEAD_ROWS = 96
AHEAD_CAST = 6
AHEAD_TRANSPOSE = 5
AHEAD_SCALE = 4
AHEAD_QUANT = 2
LAST_SCALE_ROUND = PAIRS - AHEAD_SCALE - 1
G_MORE = 160
G_ROWS = G_MORE // 4
ROOT_ROUNDS = (12, 14)
LATE = PAIRS - 1
PREP = tuple(range(PAIRS - 5)) + (LATE,) + tuple(range(PAIRS - 5, LATE))
LATE_ROUND = PAIRS - 5
CHUNKS = D // P
WARM_MATMULS = 6


def tile_candidateaware_clickednewsattention_pa_t_kernel(
    tc, cand_topics_bytes, cand_topics_scale, Wq, bq, out_0, out_1
):
    nc = tc.nc
    with ExitStack() as ctx:
        const = ctx.enter_context(tc.tile_pool(name="const", bufs=1))
        xs_pool = ctx.enter_context(tc.tile_pool(name="xs_pool", bufs=10))
        xg_head = ctx.enter_context(tc.tile_pool(name="xg_head", bufs=2))
        xg_pool = ctx.enter_context(tc.tile_pool(name="xg_pool", bufs=2))
        xq_pool = ctx.enter_context(tc.tile_pool(name="xq_pool", bufs=5))
        q_pool = ctx.enter_context(tc.tile_pool(name="q_pool", bufs=5))
        junk_pool = ctx.enter_context(tc.tile_pool(name="junk_pool", bufs=3))
        psum_t = ctx.enter_context(tc.psum_pool(name="psum_t", bufs=4))
        psum_a = ctx.enter_context(tc.psum_pool(name="psum_a", bufs=4))
        xr_pool = ctx.enter_context(tc.tile_pool(name="xr_pool", bufs=3))
        ctx.enter_context(tc.manual_schedule())

        sc8 = const.tile([P, 8], F32, name="sc8")
        nc.scalar.dma_start(
            out=sc8[:].rearrange("p (g t) -> p g t", t=4),
            in_=cand_topics_scale.rearrange("a b (g p t) -> p (a b g) t", g=2, p=P, t=4),
        )
        xbytes = []
        where = []
        for c, n in enumerate(X_LOADS):
            t = const.tile([P, n, K], U8, name="xbytes%d" % c)
            xbytes.append(t)
            for i in range(n):
                where.append((c, i))
        wraw = []
        for c in range(4):
            t = const.tile([P, 2, K], BF16, name="wraw%d" % c)
            wraw.append(t)
        bias_bc = const.tile([P, D], BF16, name="bias_bc")

        def load_x(c):
            b0 = sum(X_LOADS[:c])
            nc.sync.dma_start(
                out=xbytes[c][:],
                in_=cand_topics_bytes[b0 : b0 + X_LOADS[c]].rearrange("b n k -> n b k"),
            )

        def load_w(c):
            nc.sync.dma_start(
                out=wraw[c][:],
                in_=Wq[256 * c : 256 * (c + 1), :].rearrange("(c p) k -> p c k", p=P),
            )

        load_x(0)
        load_x(1)
        load_x(2)
        load_w(0)
        load_w(1)
        load_x(3)
        load_w(2)
        load_w(3)
        load_x(4)
        nc.sync.dma_start(out=bias_bc[:], in_=bq.partition_broadcast(P))
        load_x(5)

        ident = const.tile([P, P], F32, name="ident")
        masks.make_identity(nc, ident[:])
        ident_bf = const.tile([P, P], BF16, name="ident_bf")
        masks.make_identity(nc, ident_bf[:])
        one_col = const.tile([P, 1], F32, name="one_col")
        nc.vector.memset(one_col[:], 1.0)
        ones_bf = const.tile([P, BANK], BF16, name="ones_bf")
        nc.vector.memset(ones_bf[:], 1.0)
        for i in range(WARM_MATMULS):
            acc = psum_a.tile([P, BANK], F32, name="acc")
            nc.tensor.matmul(out=acc[:], lhsT=ones_bf[:, 0:P], rhs=ones_bf[:], start=True, stop=True)
        r2_all = const.tile([P, B], F32, name="r2_all")
        r_all = const.tile([P, P], F32, name="r_all")
        nc.vector.memset(r_all[:], 1.0)
        half = const.tile([P, B], F32, name="half")
        nc.vector.memset(half[:], 0.5)
        warm = const.tile([P, 1], F32, name="warm")
        nc.scalar.activation(out=warm[:], in_=one_col[:], func=ACT.Exp)
        sck = const.tile([P, K + G_MORE], F32, name="sck")
        nc.vector.tensor_copy(
            out=sck[:, 0:K].rearrange("p (g r t) -> p g r t", g=2, t=4),
            in_=sc8[:].rearrange("p (g t) -> p g t", t=4).unsqueeze(2).to_broadcast([P, 2, P, 4]),
        )
        nc.vector.tensor_copy(
            out=sck[:, K : K + G_MORE].rearrange("p (r t) -> p r t", t=4),
            in_=sc8[:, 0:4].unsqueeze(1).to_broadcast([P, G_ROWS, 4]),
        )

        sck_g = const.tile([P, K + G_MORE], F32, name="sck_g")

        def build_sck_g():
            nc.vector.tensor_copy(out=sck_g[:], in_=sck[:])

        wgrp = []
        wc = []
        wsc = []
        for h in range(2):
            t = const.tile([P, 4 * K], BF16, name="wgrp%d" % h, align_bytes=64)
            wgrp.append(t)
            t = const.tile([P, K], U32, name="wc%d" % h, align_bytes=64)
            wc.append(t)
            t = const.tile([P, K], U8, name="wsc%d" % h, align_bytes=64)
            wsc.append(t)

        def transposes(words, base, u_first, sums_bank=False):
            if sums_bank:
                tp = psum_a.tile([P, 4, P], F32, name="acc")
            else:
                tp = psum_t.tile([P, 4, P], F32, name="tp")
            for s in range(4):
                if u_first:
                    u, g = divmod(s, 2)
                else:
                    g, u = divmod(s, 2)
                lo = base + 256 * g
                nc.tensor.transpose(tp[:, s, :], words[:, lo + u : lo + 256 : 2], ident[:])
            return tp

        def w_transpose(c):
            h, cc = divmod(c, 4)
            tp = transposes(wraw[c // 2][:, c % 2, :].bitcast(F32), 0, False, True)
            dst = wgrp[h][:].bitcast(F32).rearrange("p (g r u) -> p g r u", g=2, u=2)
            nc.scalar.copy(
                out=dst[:, :, cc * P : (cc + 1) * P, :],
                in_=tp[:].rearrange("p (g u) r -> p g r u", u=2),
            )

        def w_quantize(h):
            nc.vector.quantize_mx(out=wc[h][:].bitcast(FP8X4), scales=wsc[h][:], in_=wgrp[h][:])

        xs_of = {}
        tp_of = {}
        xr_of = {}
        xg_of = {}
        xq_of = {}
        acc_of = {}
        q_of = {}

        def pair_bytes(j):
            c, i = where[2 * j]
            return xbytes[c][:, i : i + 2, :].rearrange("p b k -> p (b k)").bitcast(FP8)

        def new_xg(j):
            pool = xg_head if j < 2 else xg_pool
            xg = pool.tile([P, 2 * K], BF16, name="xg", align_bytes=64)
            xg_of[j] = xg

        def cast(j):
            xs = xs_pool.tile([P, 2 * K], BF16, name="xs", align_bytes=64)
            xs_of[j] = xs
            nc.scalar.copy(out=xs[:], in_=pair_bytes(j))

        def cast_transpose(j):
            words = xs_of[j][:].bitcast(F32)
            tp_of[j] = [transposes(words, 512 * a, a == 1) for a in range(2)]

        def copy_unscaled(j):
            xr = xr_pool.tile([P, K + G_MORE], BF16, name="xr", align_bytes=64)
            xr_of[j] = xr
            nc.scalar.copy(
                out=xr[:, 0:K].bitcast(F32).rearrange("p (g r u) -> p g r u", g=2, u=2),
                in_=tp_of[j][0][:].rearrange("p (g u) r -> p g r u", u=2),
            )
            nc.scalar.copy(
                out=xr[:, K : K + G_MORE].bitcast(F32).rearrange("p (r u) -> p r u", u=2),
                in_=tp_of[j][1][:, 0:4:2, 0:G_ROWS].rearrange("p u r -> p r u"),
            )

        def gpsimd_product(j):
            nc.gpsimd.tensor_tensor(
                out=xg_of[j][:, 0 : K + G_MORE], in0=xr_of[j][:], in1=sck_g[:], op=ALU.mult
            )

        def vector_product(j):
            nc.vector.tensor_tensor(
                out=xg_of[j][:, K + G_MORE : 2 * K].rearrange("p (m u e) -> p m u e", u=2, e=2),
                in0=sck[:, G_MORE:K].rearrange("p (m u e) -> p m u e", u=2, e=2),
                in1=tp_of[j][1][:]
                .rearrange("p s r -> p (s r)")
                .bitcast(BF16)
                .rearrange("p (u m e) -> p m u e", u=2, e=2)[:, G_ROWS : 2 * P],
                op=ALU.mult,
            )

        def head_cast(j, a):
            xs = xs_pool.tile([P, K], BF16, name="xs", align_bytes=64)
            xs_of[(j, a)] = xs
            c, i = where[2 * j + a]
            if (j, a) == (0, 1):
                nc.vector.tensor_copy(out=xs[:], in_=xbytes[c][:, i, :].bitcast(FP8))
            else:
                nc.scalar.copy(out=xs[:], in_=xbytes[c][:, i, :].bitcast(FP8))

        def head_transpose(j, a):
            tp_of[(j, a)] = transposes(xs_of[(j, a)][:].bitcast(F32), 0, True)

        def head_copy(j):
            xr = xr_pool.tile([P, K + G_MORE], BF16, name="xr", align_bytes=64)
            xr_of[j] = xr
            nc.scalar.copy(
                out=xr[:, 0 : 4 * HEAD_ROWS].bitcast(F32).rearrange("p (m u) -> p m u", u=2),
                in_=tp_of[(j, 1)][:].rearrange("p s r -> p (s r)").rearrange("p (u m) -> p m u", u=2)[:, 0:HEAD_ROWS, :],
            )

        def head_gpsimd(j):
            n = 4 * HEAD_ROWS
            nc.gpsimd.tensor_tensor(out=xg_of[j][:, K : K + n], in0=xr_of[j][:, 0:n], in1=sck_g[:, 0:n], op=ALU.mult)

        def head_vector(j, a):
            m0 = HEAD_ROWS if a == 1 else 0
            nc.vector.tensor_tensor(
                out=xg_of[j][:, a * K + 4 * m0 : (a + 1) * K].rearrange("p (m u e) -> p m u e", u=2, e=2),
                in0=sck[:, 4 * m0 : K].rearrange("p (m u e) -> p m u e", u=2, e=2),
                in1=tp_of[(j, a)][:]
                .rearrange("p s r -> p (s r)")
                .bitcast(BF16)
                .rearrange("p (u m e) -> p m u e", u=2, e=2)[:, m0 : 2 * P],
                op=ALU.mult,
            )

        def quantize(j):
            xc = xq_pool.tile([P, 512], U32, name="xc", align_bytes=64)
            xsc = xq_pool.tile([P, 512], U8, name="xsc", align_bytes=64)
            xq_of[j] = (xc, xsc)
            nc.vector.quantize_mx(out=xc[:].bitcast(FP8X4), scales=xsc[:], in_=xg_of[j][:])

        def multiply(j, s):
            a, h = divmod(s, 2)
            xc, xsc = xq_of[j]
            acc = psum_a.tile([P, BANK], F32, name="acc")
            acc_of[(j, s)] = acc
            for g in range(2):
                c0 = (2 * a + g) * P
                nc.tensor.matmul_mx(
                    out=acc[:],
                    lhsT=xc[:, c0 : c0 + P].bitcast(FP8X4),
                    lhsT_scale=xsc[:, c0 : c0 + P],
                    rhs=wc[h][:, g * BANK : (g + 1) * BANK].bitcast(FP8X4),
                    rhs_scale=wsc[h][:, g * BANK : (g + 1) * BANK],
                    start=(g == 0),
                    stop=(g == 1),
                )

        def add_bias(j, s):
            a, h = divmod(s, 2)
            if h == 0:
                q = q_pool.tile([P, D], F32, name=("qa", "qb")[a])
                q_of[(j, a)] = q
            nc.vector.tensor_tensor(
                out=q_of[(j, a)][:, h * BANK : (h + 1) * BANK],
                in0=bias_bc[:, h * BANK : (h + 1) * BANK],
                in1=acc_of[(j, s)][:],
                op=ALU.add,
            )

        def sum_squares(j, a):
            b = 2 * j + a
            junk = junk_pool.tile([P, D], BF16, name="junk")
            nc.scalar.activation(
                out=junk[:], in_=q_of[(j, a)][:], func=ACT.Square, accum_out=r2_all[:, b : b + 1]
            )

        def roots(lo, hi):
            nc.gpsimd.tensor_tensor(
                out=r_all[:, lo:hi], in0=r2_all[:, lo:hi], in1=half[:, 0 : hi - lo], op=ALU.pow
            )

        def store(j, a):
            nc.sync.dma_start(out=out_0[2 * j + a], in_=q_of[(j, a)][:])

        sq_late = const.tile([P, CHUNKS, 2 * P], F32, name="sq_late")
        late_bank = {}
        bias_col = const.tile([P, CHUNKS], F32, name="bias_col")

        def turn_bias():
            tp = psum_t.tile([P, 4, P], F32, name="tp")
            turned = tp[:].rearrange("p s r -> p (s r)").bitcast(BF16)
            for c in range(CHUNKS):
                nc.tensor.transpose(turned[:, c * P : (c + 1) * P], bias_bc[:, c * P : (c + 1) * P], ident_bf[:])
            nc.scalar.copy(out=bias_col[:], in_=turned.rearrange("p (c r) -> p c r", r=P)[:, :, 0])

        def late_multiply(i):
            xc, xsc = xq_of[LATE]
            tp = psum_t.tile([P, 4, P], F32, name="tp")
            late_bank[i] = tp
            for e in range(2):
                h, cc = divmod(2 * i + e, 4)
                for a in range(2):
                    for g in range(2):
                        w0 = g * BANK + cc * P
                        c0 = (2 * a + g) * P
                        nc.tensor.matmul_mx(
                            out=tp[:, 2 * e + a, :],
                            lhsT=wc[h][:, w0 : w0 + P].bitcast(FP8X4),
                            lhsT_scale=wsc[h][:, w0 : w0 + P],
                            rhs=xc[:, c0 : c0 + P].bitcast(FP8X4),
                            rhs_scale=xsc[:, c0 : c0 + P],
                            start=(g == 0),
                            stop=(g == 1),
                        )

        def late_square(i):
            for e in range(2):
                c = 2 * i + e
                nc.scalar.activation(
                    out=sq_late[:, c, :],
                    in_=late_bank[i][:, 2 * e : 2 * e + 2, :].rearrange("p a r -> p (a r)"),
                    func=ACT.Square,
                    bias=bias_col[:, c : c + 1],
                    scale=1.0,
                )

        def late_sum_blocks(i):
            if i == 0:
                for a in range(2):
                    tp = psum_t.tile([P, 4, P], F32, name="tp")
                    late_bank[("sum", a)] = tp
            for e in range(2):
                c = 2 * i + e
                for a in range(2):
                    nc.tensor.matmul(
                        out=late_bank[("sum", a)][:, 0, :],
                        lhsT=sq_late[:, c, a * P : (a + 1) * P],
                        rhs=ident[:],
                        is_transpose=True,
                        start=(c == 0),
                        stop=(c == CHUNKS - 1),
                    )

        def late_sum_columns():
            for a in range(2):
                b = 2 * LATE + a
                junk = junk_pool.tile([P, D], BF16, name="junk")
                nc.scalar.activation(
                    out=junk[:, 0:P], in_=late_bank[("sum", a)][:, 0, :], func=ACT.Copy, accum_out=r2_all[:, b : b + 1]
                )

        for j in range(HEAD_PAIRS):
            new_xg(j)
        head_cast(0, 0)
        head_transpose(0, 0)
        head_cast(0, 1)
        build_sck_g()
        head_transpose(0, 1)
        head_cast(1, 0)
        head_transpose(1, 0)
        head_cast(1, 1)
        head_vector(0, 0)
        head_copy(0)
        head_gpsimd(0)
        head_vector(0, 1)
        head_transpose(1, 1)
        head_cast(2, 0)
        head_cast(2, 1)
        head_vector(1, 0)
        head_copy(1)
        head_gpsimd(1)
        head_vector(1, 1)
        w_transpose(0)
        head_transpose(2, 0)
        head_transpose(2, 1)
        head_cast(3, 0)
        head_vector(2, 0)
        head_copy(2)
        head_gpsimd(2)
        head_vector(2, 1)
        head_cast(3, 1)
        w_transpose(1)
        head_transpose(3, 0)
        head_transpose(3, 1)
        head_vector(3, 0)
        head_copy(3)
        head_gpsimd(3)
        head_vector(3, 1)
        w_transpose(2)
        w_transpose(3)
        cast(HEAD_PAIRS)
        for c in range(4, 8):
            w_transpose(c)
        w_quantize(0)
        quantize(0)
        cast_transpose(HEAD_PAIRS)
        copy_unscaled(HEAD_PAIRS)
        quantize(1)
        w_quantize(1)
        cast(HEAD_PAIRS + 1)
        for s in range(4):
            multiply(0, s)

        ex = const.tile([P, P], F32, name="ex")
        ex_sum = const.tile([P, 1], F32, name="ex_sum")

        def softmax_head():
            rt = psum_t.tile([P, 4, P], F32, name="tp")
            r_rows = rt[:, 0, :]
            nc.tensor.transpose(r_rows, r_all[:], ident[:])
            neg_max = const.tile([P, 1], F32, name="neg_max")
            nc.vector.reduce_max(out=neg_max[:], in_=r_rows, axis=AX.X, negate=True)
            nc.scalar.activation(
                out=ex[:], in_=r_rows, func=ACT.Exp, bias=neg_max[:], scale=1.0, accum_out=ex_sum[:]
            )

        def softmax_end():
            inv_sum = const.tile([P, 1], F32, name="inv_sum")
            nc.vector.reciprocal(out=inv_sum[:], in_=ex_sum[:])
            weights = const.tile([P, P], F32, name="weights")
            nc.vector.tensor_scalar(
                out=weights[:], in0=ex[:], scalar1=inv_sum[:], scalar2=None, op0=ALU.mult
            )
            nc.sync.dma_start(out=out_1[:, :], in_=weights[0:B, :])

        def store_bank(j, s):
            a, h = divmod(s, 2)
            nc.sync.dma_start(
                out=out_0[2 * j + a][:, h * BANK : (h + 1) * BANK], in_=q_of[(j, a)][:, h * BANK : (h + 1) * BANK]
            )

        rooted = 0
        for c in range(PAIRS):
            if c <= LAST_SCALE_ROUND:
                quantize(PREP[c + AHEAD_QUANT])
                new_xg(PREP[c + AHEAD_SCALE])
                gpsimd_product(PREP[c + AHEAD_SCALE])
            elif c == LAST_SCALE_ROUND + 1:
                for i in range(c + AHEAD_QUANT, PAIRS):
                    quantize(PREP[i])
            if 0 < c < LATE:
                sum_squares(c - 1, 1)
            if c == LATE_ROUND - 1:
                late_square(0)
            if c == LATE_ROUND:
                late_square(1)
            if c == LATE_ROUND + 1:
                late_sum_blocks(3)
                late_sum_columns()
            if c in ROOT_ROUNDS:
                roots(rooted, 2 * c)
                rooted = 2 * c
            if c == LATE - 1:
                roots(2 * LATE, B)
            if c + AHEAD_CAST < PAIRS:
                cast(PREP[c + AHEAD_CAST])
            if c + AHEAD_TRANSPOSE < PAIRS:
                cast_transpose(PREP[c + AHEAD_TRANSPOSE])
                copy_unscaled(PREP[c + AHEAD_TRANSPOSE])
            if c == LATE_ROUND - 3:
                turn_bias()
            if c == LATE_ROUND:
                late_multiply(2)
                late_multiply(3)
                late_square(2)
            for s in range(4):
                add_bias(c, s)
                if c + 1 < PAIRS:
                    multiply(c + 1, s)
                if s == 0 and c <= LAST_SCALE_ROUND:
                    vector_product(PREP[c + AHEAD_SCALE])
                if s == 0 and c == LATE_ROUND - 2:
                    late_multiply(0)
                if s == 0 and c == LATE_ROUND - 1:
                    late_multiply(1)
                if s == 0 and c == LATE_ROUND:
                    for i in range(3):
                        late_sum_blocks(i)
                if c == LATE:
                    store_bank(c, s)
                elif s % 2 == 1:
                    store(c, s // 2)
                if c == LATE and s == 3:
                    softmax_head()
            if c < LATE:
                sum_squares(c, 0)
            if c == LATE_ROUND:
                late_square(3)
            if c == LATE - 1:
                roots(rooted, 2 * LATE - 1)
                sum_squares(LATE - 1, 1)
                roots(2 * LATE - 1, 2 * LATE)
        softmax_end()
